import numpy as np
import ml_dtypes


def mxq(x, axis, fmt="e4m3"):
    dtype, down = {"e4m3": (ml_dtypes.float8_e4m3fn, 7), "e5m2": (ml_dtypes.float8_e5m2, 14)}[fmt]
    v = np.moveaxis(np.asarray(x, np.float32).astype(ml_dtypes.bfloat16).astype(np.float64), axis, -1)
    blocks = v.reshape(v.shape[:-1] + (-1, 32))
    amax = np.abs(blocks).max(-1, keepdims=True)
    byte = np.maximum(np.where(amax > 0, np.frexp(amax)[1] - 1 + 127, 0) - down, 1)
    scale = np.exp2(byte - 127.0)
    codes = (blocks / scale).astype(np.float32).astype(dtype).astype(np.float64)
    return np.moveaxis((codes * scale).reshape(v.shape), -1, axis)


WIDE = False


def mx_kscale(k):
    if not WIDE:
        return np.ones(k)
    levels = np.array([10, -10, 5, -5, 0])
    a = np.random.permutation(np.resize(levels, k // 512 * 4)).reshape(k // 512, 4)
    idx = np.arange(k)
    return np.exp2(a[idx // 512, idx % 128 // 32])


BF16 = ml_dtypes.bfloat16


def bf(x):
    return np.asarray(x, np.float32).astype(BF16)


def f64(x):
    return np.asarray(x).astype(np.float64)


B, I, H, ORDER = 1024, 512, 512, 3
MASK = 1.0 - 0.2


def sigmoid(v):
    return 1.0 / (1.0 + np.exp(-v))


def setup_inputs():
    s = mx_kscale(I)
    return {"x": bf(np.random.standard_normal((B, I)) * s),
            "h": bf(np.random.standard_normal((B, H))),
            "c": bf(np.random.standard_normal((B, H))),
            "mem_read": bf(np.random.standard_normal((B, H)) * 0.55),
            "W_ih": bf(np.random.standard_normal((I, 4 * H)) * 0.7 / np.sqrt(I) / s[:, None]),
            "W_hh": bf(np.random.standard_normal((H, 4 * H)) * 0.7 / np.sqrt(H)),
            "bias": bf(np.random.standard_normal(4 * H) * 0.3)}


def reference(x, h, c, mem_read, W_ih, W_hh, bias):
    h0, c0 = f64(h), f64(c)
    gates = ((mxq(f64(x), 1, "e4m3") @ mxq(f64(W_ih), 0, "e4m3"))
             + (mxq(h0, 1, "e4m3") @ mxq(f64(W_hh), 0, "e4m3"))
             + f64(bias))
    f, i, o, g = np.split(gates, 4, axis=1)
    c_next = sigmoid(f) * c0 + sigmoid(i) * np.tanh(g) + f64(mem_read)
    h_next = sigmoid(o) * np.tanh(c_next)
    h_next = h_next * MASK + h0 * (1.0 - MASK)
    c_next = c_next * MASK + c0 * (1.0 - MASK)
    return h_next, c_next

@@ -1,0 +1,263 @@
+from contextlib import ExitStack
+
+import concourse.mybir as mybir
+from concourse.masks import make_identity
+
+F32 = mybir.dt.float32
+BF16 = mybir.dt.bfloat16
+U32 = mybir.dt.uint32
+U8 = mybir.dt.uint8
+FP8X4 = mybir.dt.float8_e4m3fn_x4
+ACT = mybir.ActivationFunctionType
+ALU = mybir.AluOpType
+
+P = 128
+B, K, H = 1024, 512, 512
+FLOPS = 2 * B * (2 * K) * (4 * H)
+TPC = 4
+GATE_F, GATE_I, GATE_O, GATE_G = 0, 1, 2, 3
+FUNC = {GATE_F: ACT.Sigmoid, GATE_I: ACT.Sigmoid, GATE_O: ACT.Sigmoid, GATE_G: ACT.Tanh}
+ACT_BUFS = {GATE_F: 2, GATE_I: 5, GATE_G: 2, GATE_O: 2}
+PINNED = True
+STEPS = (
+    ("setup",), ("ld", 0, 0), ("ld", 1, 0), ("ldW", 0, 0), ("ldW", 0, 1), ("biasT",), ("xt", 0, 0, 0), ("ld", 2, 0),
+    ("xcp", 0, 0, 0, "S"), ("xt", 0, 0, 1), ("xcp", 0, 0, 1, "S"), ("xt", 1, 0, 1), ("xq", 0, 0), ("ldW", 1, 0),
+    ("rg", 0, 0, "V"), ("ldW", 1, 1), ("xt", 1, 0, 0), ("xcp", 1, 0, 1, "S"), ("xcp", 1, 0, 0, "S"), ("xq", 1, 0),
+    ("wq", 0, 0), ("mxa", 0, 0, 0), ("rg", 1, 0, "V"), ("mxa", 0, 1, 0), ("wq", 1, 0), ("mxb", 0, 0, 0),
+    ("act", 0, 0, 0), ("rg", 0, 1, "V"), ("ldW", 3, 0), ("ldW", 3, 1), ("mxa", 0, 2, 0), ("ct", 0, 0),
+    ("mxb", 0, 2, 0), ("mxa", 0, 3, 0), ("wq", 0, 1), ("ld", 3, 0), ("mxb", 0, 1, 0), ("mxa", 0, 1, 1),
+    ("act", 0, 1, 0), ("a", 0, 0), ("rg", 1, 1, "V"), ("ct", 0, 1), ("a", 0, 1), ("mxb", 0, 3, 0), ("wq", 1, 1),
+    ("act", 0, 2, 0), ("mxa", 0, 2, 1), ("rg", 0, 3, "V"), ("ldW", 2, 0), ("act", 0, 3, 0), ("mxa", 0, 0, 1),
+    ("mxb", 0, 2, 1), ("mxb", 0, 0, 1), ("ldW", 2, 1), ("mxb", 0, 1, 1), ("mxa", 0, 3, 1), ("ct", 0, 2),
+    ("act", 0, 1, 1), ("mxb", 0, 3, 1), ("act", 0, 2, 1), ("wq", 0, 3), ("act", 0, 3, 1), ("ld", 0, 1), ("a", 0, 2),
+    ("rg", 1, 3, "V"), ("wq", 1, 3), ("mxa", 0, 1, 3), ("ct", 0, 3), ("mxa", 0, 0, 3), ("mxa", 0, 2, 3),
+    ("act", 0, 0, 1), ("a", 0, 3), ("c02", 0, "V", 2), ("ld", 1, 1), ("c02", 0, "V", 3), ("mxa", 0, 3, 3),
+    ("rg", 1, 2, "S", 1, 4), ("rg", 0, 2, "V"), ("wq", 0, 2), ("mxb", 0, 1, 3), ("rg", 1, 2, "S", 3, 4),
+    ("xt", 0, 1, 0), ("rg", 1, 2, "S", 2, 4), ("act", 0, 1, 3), ("ld", 2, 1), ("mxb", 0, 0, 3), ("mxb", 0, 2, 3),
+    ("xcp", 0, 1, 0, "S"), ("rg", 1, 2, "S", 0, 4), ("ld", 3, 1), ("mxb", 0, 3, 3), ("xt", 0, 1, 1),
+    ("act", 0, 0, 3), ("wq", 1, 2), ("b", 0, 0, "V"), ("ct", 1, 0), ("mxa", 0, 0, 2), ("mxa", 0, 1, 2),
+    ("b", 0, 1, "V"), ("c02", 0, "V", 0), ("mxb", 0, 0, 2), ("xcp", 0, 1, 1, "S"), ("act", 0, 0, 2),
+    ("mxb", 0, 1, 2), ("xt", 1, 1, 0), ("act", 0, 2, 3), ("act", 0, 3, 3), ("tz", 0, 0), ("cnx", 0, 0),
+    ("mxa", 0, 2, 2), ("b", 0, 2, "V"), ("mxb", 0, 2, 2), ("mxa", 0, 3, 2), ("mxb", 0, 3, 2), ("tz", 0, 1),
+    ("tc", 0, 0), ("xq", 0, 1), ("xt", 1, 1, 1), ("c02", 0, "V", 1), ("to", 0, 0), ("tz", 0, 2), ("mxa", 1, 0, 0),
+    ("cnx", 0, 1), ("b", 0, 3, "V"), ("xcp", 1, 1, 0, "S"), ("tc", 0, 1), ("xcp", 1, 1, 1, "S"), ("mxa", 1, 0, 1),
+    ("act", 0, 1, 2), ("tc", 0, 2), ("xq", 1, 1), ("mxb", 1, 0, 0), ("tz", 0, 3), ("act", 0, 2, 2), ("act", 1, 0, 0),
+    ("cnx", 0, 2), ("act", 0, 3, 2), ("p8", 0, 0), ("to", 0, 1), ("mxb", 1, 0, 1), ("act", 1, 0, 1), ("hnx", 0, 0),
+    ("mxa", 1, 0, 3), ("mxb", 1, 0, 3), ("mxa", 1, 1, 0), ("cnx", 0, 3), ("mxa", 1, 1, 3), ("mxb", 1, 1, 0),
+    ("mxb", 1, 1, 3), ("mxa", 1, 0, 2), ("act", 1, 0, 3), ("to", 0, 2), ("tc", 0, 3), ("mxa", 1, 1, 1),
+    ("act", 1, 1, 3), ("mxb", 1, 1, 1), ("c02", 1, "V", 2), ("p8", 0, 1), ("hnx", 0, 1), ("mxb", 1, 0, 2),
+    ("act", 1, 1, 0), ("st", 0, "c", 0, 4), ("c02", 1, "V", 3), ("mxa", 1, 1, 2), ("act", 1, 1, 1), ("b", 1, 0, "V"),
+    ("a", 1, 0), ("mxa", 1, 2, 0), ("p8", 0, 2), ("mxb", 1, 1, 2), ("to", 0, 3), ("tz", 1, 0), ("act", 1, 0, 2),
+    ("hnx", 0, 2), ("c02", 1, "V", 0), ("to", 1, 0), ("ct", 1, 1), ("c02", 1, "V", 1), ("p8", 0, 3), ("hnx", 0, 3),
+    ("mxa", 1, 2, 2), ("mxb", 1, 2, 0), ("mxb", 1, 2, 2), ("mxa", 1, 2, 1), ("b", 1, 1, "V"), ("act", 1, 1, 2),
+    ("a", 1, 1), ("mxb", 1, 2, 1), ("tc", 1, 0), ("mxa", 1, 2, 3), ("cnx", 1, 0), ("tz", 1, 1), ("act", 1, 2, 2),
+    ("to", 1, 1), ("ct", 1, 2), ("p8", 1, 0), ("mxb", 1, 2, 3), ("act", 1, 2, 0), ("hnx", 1, 0), ("cnx", 1, 1),
+    ("tc", 1, 1), ("a", 1, 2), ("mxa", 1, 3, 3), ("mxb", 1, 3, 3), ("act", 1, 2, 1), ("mxa", 1, 3, 0),
+    ("mxa", 1, 3, 1), ("mxb", 1, 3, 1), ("p8", 1, 1), ("mxb", 1, 3, 0), ("act", 1, 2, 3), ("b", 1, 2, "V"),
+    ("tz", 1, 2), ("act", 1, 3, 3), ("ct", 1, 3), ("to", 1, 2), ("act", 1, 3, 1), ("act", 1, 3, 0), ("hnx", 1, 1),
+    ("mxa", 1, 3, 2), ("tc", 1, 2), ("b", 1, 3, "V"), ("cnx", 1, 2), ("a", 1, 3), ("st", 0, "h", 0, 4), ("p8", 1, 2),
+    ("mxb", 1, 3, 2), ("hnx", 1, 2), ("act", 1, 3, 2), ("tz", 1, 3), ("tc", 1, 3), ("to", 1, 3), ("p8", 1, 3),
+    ("st", 1, "c", 0, 3), ("st", 1, "h", 0, 3), ("cnx", 1, 3), ("hnx", 1, 3), ("st", 1, "c", 3, 4),
+    ("st", 1, "h", 3, 4),
+)
+
+
+def tile_lstmcell_pb_kernel(tc, x, h, c, mem_read, W_ih, W_hh, bias, out_0, out_1):
+    nc = tc.nc
+    with ExitStack() as ctx:
+        const = ctx.enter_context(tc.tile_pool(name="const", bufs=1))
+        inp = ctx.enter_context(tc.tile_pool(name="inp", bufs=1))
+        wrawp = ctx.enter_context(tc.tile_pool(name="wraw", bufs=1))
+        wgp = ctx.enter_context(tc.tile_pool(name="wg", bufs=4))
+        agp = ctx.enter_context(tc.tile_pool(name="ag", bufs=2))
+        codes = ctx.enter_context(tc.tile_pool(name="codes", bufs=1))
+        work = ctx.enter_context(tc.tile_pool(name="work", bufs=2))
+        stage = ctx.enter_context(tc.tile_pool(name="stage", bufs=2))
+        psum = ctx.enter_context(tc.psum_pool(name="psum", bufs=1))
+        if PINNED:
+            ctx.enter_context(tc.manual_schedule())
+
+        views = [t.rearrange("(p r) k -> p r k", r=2 * TPC) for t in (x, h, c, mem_read)]
+        outv = {"h": out_0.rearrange("(p r) k -> p r k", r=2 * TPC), "c": out_1.rearrange("(p r) k -> p r k", r=2 * TPC)}
+        weights = (W_ih, W_hh)
+        T = {}
+
+        def engine(e):
+            return {"V": nc.vector, "S": nc.scalar, "G": nc.gpsimd}[e]
+
+        def ld(which, n):
+            t = inp.tile([P, TPC, K], BF16, name="in%d%d" % (which, n))
+            nc.sync.dma_start(out=t[:], in_=views[which][:, TPC * n:TPC * (n + 1), :])
+            T[("in", which, n)] = t
+
+        def ldW(gate, w):
+            t = wrawp.tile([P, 4, H], BF16, name="wraw%d%d" % (w, gate))
+            for u in range(2):
+                nc.sync.dma_start(
+                    out=t[:, 2 * u:2 * u + 2, :],
+                    in_=weights[w][256 * u:256 * (u + 1), H * gate:H * (gate + 1)].rearrange("(p e) c -> p e c", e=2),
+                )
+            T[("wraw", w, gate)] = t
+
+        def setup():
+            bz = const.tile([P, P], BF16, name="bz")
+            nc.vector.memset(bz[:], 0.0)
+            nc.scalar.dma_start(out=bz[0:16, :], in_=bias.rearrange("(t m) -> t m", m=P))
+            ident_f = const.tile([P, P], F32, name="ident_f")
+            make_identity(nc, ident_f[:])
+            ident_b = const.tile([P, P], BF16, name="ident_b")
+            make_identity(nc, ident_b[:])
+            T["bz"] = bz
+            T["if"] = ident_f
+            T["ib"] = ident_b
+
+        def biasT():
+            bt = psum.tile([P, P], BF16, name="bt", tag="sp")
+            nc.tensor.transpose(bt[:], T["bz"][:], T["ib"][:])
+            t = const.tile([P, 16], F32, name="biasT")
+            nc.vector.tensor_copy(out=t[:], in_=bt[:, 0:16])
+            T["bias"] = t
+
+        def xt(o, n, q):
+            if n == 0:
+                pt = psum.tile([P, 4, P], F32, name="pt%d%d%d" % (o, n, q), tag="acc", bufs=4)
+            else:
+                pt = psum.tile([P, 4, P], F32, name="pt%d%d%d" % (o, n, q), tag="sp")
+            src32 = T[("in", o, n)][:].bitcast(F32)
+            for rr in range(2):
+                for u in range(2):
+                    nc.tensor.transpose(pt[:, 2 * rr + u, :], src32[:, 2 * q + rr, P * u:P * (u + 1)], T["if"][:])
+            T[("pt", o, n, q)] = pt
+
+        def xcp(o, n, q, e):
+            if ("ag", o, n) not in T:
+                T[("ag", o, n)] = agp.tile([P, 4 * TPC * P], BF16, name="ag%d%d" % (o, n), tag="ag", align_bytes=64)
+            dst = T[("ag", o, n)][:].bitcast(F32)[:, 512 * q:512 * (q + 1)].rearrange("p (rr b u) -> p rr b u", rr=2, u=2)
+            src = T[("pt", o, n, q)][:].rearrange("p (rr u) b -> p rr b u", u=2)
+            if e == "V":
+                nc.vector.tensor_copy(out=dst, in_=src)
+            else:
+                nc.scalar.copy(out=dst, in_=src)
+
+        def xq(o, n):
+            cd = codes.tile([P, TPC * P], U32, name="acode%d%d" % (o, n), align_bytes=64)
+            sc = codes.tile([P, TPC * P], U8, name="ascale%d%d" % (o, n), align_bytes=64)
+            nc.vector.quantize_mx(out=cd[:].bitcast(FP8X4), scales=sc[:], in_=T[("ag", o, n)][:])
+            T[("ac", o, n)] = (cd, sc)
+
+        def rg(w, gate, e, part=0, nparts=1):
+            if ("wg", w, gate) not in T:
+                T[("wg", w, gate)] = wgp.tile([P, H, 4], BF16, name="wg%d%d" % (w, gate), tag="wg", align_bytes=64)
+            width = H // nparts
+            cols = slice(width * part, width * (part + 1))
+            dst = T[("wg", w, gate)][:, cols, :].rearrange("p (cc i) t -> p cc t i", i=4)
+            src = T[("wraw", w, gate)][:, :, cols].rearrange("p t (cc i) -> p cc t i", i=4)
+            if e == "V":
+                nc.vector.tensor_copy(out=dst, in_=src)
+            else:
+                nc.scalar.copy(out=dst, in_=src)
+
+        def wq(w, gate):
+            cd = codes.tile([P, H], U32, name="wcode%d%d" % (w, gate), align_bytes=64)
+            sc = codes.tile([P, H], U8, name="wscale%d%d" % (w, gate), align_bytes=64)
+            nc.vector.quantize_mx(out=cd[:].bitcast(FP8X4), scales=sc[:], in_=T[("wg", w, gate)][:].rearrange("p cm t -> p (cm t)"))
+            T[("wc", w, gate)] = (cd, sc)
+
+        def mx(n, j, gate, w):
+            if w == 0:
+                T[("acc", n, j, gate)] = psum.tile([P, TPC * P], F32, name="acc", tag="acc", bufs=4)
+            wcd, wsc = T[("wc", w, gate)]
+            acd, asc = T[("ac", w, n)]
+            nc.tensor.matmul_mx(
+                out=T[("acc", n, j, gate)][:],
+                lhsT=wcd[:, P * j:P * (j + 1)].bitcast(FP8X4),
+                lhsT_scale=wsc[:, P * j:P * (j + 1)],
+                rhs=acd[:].bitcast(FP8X4),
+                rhs_scale=asc[:],
+                start=(w == 0),
+                stop=(w == 1),
+            )
+
+        def mxa(n, j, gate):
+            mx(n, j, gate, 0)
+
+        def mxb(n, j, gate):
+            mx(n, j, gate, 1)
+
+        def act(n, j, gate):
+            res = work.tile([P, TPC * P], F32, name="act%d" % gate, tag="act%d" % gate, bufs=ACT_BUFS[gate])
+            col = 4 * gate + j
+            nc.scalar.activation(out=res[:], in_=T[("acc", n, j, gate)][:], func=FUNC[gate], bias=T["bias"][:, col:col + 1], scale=1.0)
+            T[("act", n, j, gate)] = res
+
+        def c02(n, e, j):
+            t = work.tile([P, TPC, P], F32, name="c02", tag="c02", bufs=4)
+            src = T[("in", 2, n)][:, :, P * j:P * (j + 1)]
+            if e == "S":
+                nc.scalar.activation(out=t[:], in_=src, func=ACT.Copy, scale=0.2)
+            else:
+                engine(e).tensor_scalar(out=t[:], in0=src, scalar1=0.2, scalar2=0.0, op0=ALU.mult, op1=ALU.add)
+            T[("c02", n, j)] = t
+
+        def ct(n, j):
+            t = psum.tile([P, TPC * P], BF16, name="ct", tag="ct")
+            for s in range(TPC):
+                nc.tensor.transpose(t[:, P * s:P * (s + 1)], T[("in", 2, n)][:, s, P * j:P * (j + 1)], T["ib"][:])
+            T[("ct", n, j)] = t
+
+        def a(n, j):
+            t = work.tile([P, TPC * P], F32, name="pa", tag="pa", bufs=5)
+            nc.vector.tensor_tensor(out=t[:], in0=T[("act", n, j, GATE_F)][:], in1=T[("ct", n, j)][:], op=ALU.mult)
+            T[("pa", n, j)] = t
+
+        def b(n, j, e):
+            t = work.tile([P, TPC * P], F32, name="pb", tag="pb", bufs=2)
+            engine(e).tensor_tensor(out=t[:], in0=T[("act", n, j, GATE_I)][:], in1=T[("act", n, j, GATE_G)][:], op=ALU.mult)
+            T[("pb", n, j)] = t
+
+        def tz(n, j):
+            zs = psum.tile([P, TPC, P], F32, name="zs", tag="zs")
+            for s in range(TPC):
+                bcols = slice(P * s, P * (s + 1))
+                nc.tensor.matmul(zs[:, s, :], lhsT=T[("pa", n, j)][:, bcols], rhs=T["if"][:], is_transpose=True, start=True, stop=False)
+                nc.tensor.matmul(zs[:, s, :], lhsT=T[("pb", n, j)][:, bcols], rhs=T["if"][:], is_transpose=True, start=False, stop=False)
+                nc.tensor.matmul(zs[:, s, :], lhsT=T["ib"][:], rhs=T[("in", 3, n)][:, s, P * j:P * (j + 1)], start=False, stop=True)
+            T[("zs", n, j)] = zs
+
+        def tcn(n, j):
+            t = work.tile([P, TPC, P], F32, name="tcn", tag="tcn", bufs=5)
+            nc.scalar.activation(out=t[:], in_=T[("zs", n, j)][:], func=ACT.Tanh)
+            T[("tcn", n, j)] = t
+
+        def cnx(n, j):
+            if ("cst", n) not in T:
+                T[("cst", n)] = stage.tile([P, TPC, H], F32, name="cstage", tag="cstage")
+            nc.vector.scalar_tensor_tensor(out=T[("cst", n)][:, :, P * j:P * (j + 1)], in0=T[("zs", n, j)][:], scalar=0.8,
+                                           in1=T[("c02", n, j)][:], op0=ALU.mult, op1=ALU.add)
+
+        def to(n, j):
+            zo = psum.tile([P, TPC, P], F32, name="zo", tag="zo")
+            for s in range(TPC):
+                nc.tensor.transpose(zo[:, s, :], T[("act", n, j, GATE_O)][:, P * s:P * (s + 1)], T["if"][:])
+            T[("zo", n, j)] = zo
+
+        def p8(n, j):
+            t = work.tile([P, TPC, P], F32, name="p8", tag="p8")
+            nc.vector.scalar_tensor_tensor(out=t[:], in0=T[("zo", n, j)][:], scalar=0.8, in1=T[("tcn", n, j)][:], op0=ALU.mult, op1=ALU.mult)
+            T[("p8", n, j)] = t
+
+        def hnx(n, j):
+            if ("hst", n) not in T:
+                T[("hst", n)] = stage.tile([P, TPC, H], F32, name="hstage", tag="hstage")
+            nc.vector.scalar_tensor_tensor(out=T[("hst", n)][:, :, P * j:P * (j + 1)], in0=T[("in", 1, n)][:, :, P * j:P * (j + 1)], scalar=0.2,
+                                           in1=T[("p8", n, j)][:], op0=ALU.mult, op1=ALU.add)
+
+        def st(n, which, j0, j1):
+            cols = slice(P * j0, P * j1)
+            nc.sync.dma_start(out=outv[which][:, TPC * n:TPC * (n + 1), cols], in_=T[(which + "st", n)][:, :, cols])
+
+        ops = {"ld": ld, "ldW": ldW, "setup": setup, "biasT": biasT, "xt": xt, "xcp": xcp, "xq": xq, "rg": rg, "wq": wq,
+               "mxa": mxa, "mxb": mxb, "act": act, "c02": c02, "ct": ct, "a": a, "b": b, "tz": tz, "tc": tcn, "cnx": cnx,
+               "to": to, "p8": p8, "hnx": hnx, "st": st}
+        for step in STEPS:
+            ops[step[0]](*step[1:])

@@ -14,52 +14,15 @@ ALU = mybir.AluOpType
 P = 128
 B, K, H = 1024, 512, 512
 FLOPS = 2 * B * (2 * K) * (4 * H)
+
+NCHUNK = 2
 TPC = 4
+NJ = 4
 GATE_F, GATE_I, GATE_O, GATE_G = 0, 1, 2, 3
-FUNC = {GATE_F: ACT.Sigmoid, GATE_I: ACT.Sigmoid, GATE_O: ACT.Sigmoid, GATE_G: ACT.Tanh}
-ACT_BUFS = {GATE_F: 2, GATE_I: 5, GATE_G: 2, GATE_O: 2}
-PINNED = True
-STEPS = (
-    ("setup",), ("ld", 0, 0), ("ld", 1, 0), ("ldW", 0, 0), ("ldW", 0, 1), ("biasT",), ("xt", 0, 0, 0), ("ld", 2, 0),
-    ("xcp", 0, 0, 0, "S"), ("xt", 0, 0, 1), ("xcp", 0, 0, 1, "S"), ("xt", 1, 0, 1), ("xq", 0, 0), ("ldW", 1, 0),
-    ("rg", 0, 0, "V"), ("ldW", 1, 1), ("xt", 1, 0, 0), ("xcp", 1, 0, 1, "S"), ("xcp", 1, 0, 0, "S"), ("xq", 1, 0),
-    ("wq", 0, 0), ("mxa", 0, 0, 0), ("rg", 1, 0, "V"), ("mxa", 0, 1, 0), ("wq", 1, 0), ("mxb", 0, 0, 0),
-    ("act", 0, 0, 0), ("rg", 0, 1, "V"), ("ldW", 3, 0), ("ldW", 3, 1), ("mxa", 0, 2, 0), ("ct", 0, 0),
-    ("mxb", 0, 2, 0), ("mxa", 0, 3, 0), ("wq", 0, 1), ("ld", 3, 0), ("mxb", 0, 1, 0), ("mxa", 0, 1, 1),
-    ("act", 0, 1, 0), ("a", 0, 0), ("rg", 1, 1, "V"), ("ct", 0, 1), ("a", 0, 1), ("mxb", 0, 3, 0), ("wq", 1, 1),
-    ("act", 0, 2, 0), ("mxa", 0, 2, 1), ("rg", 0, 3, "V"), ("ldW", 2, 0), ("act", 0, 3, 0), ("mxa", 0, 0, 1),
-    ("mxb", 0, 2, 1), ("mxb", 0, 0, 1), ("ldW", 2, 1), ("mxb", 0, 1, 1), ("mxa", 0, 3, 1), ("ct", 0, 2),
-    ("act", 0, 1, 1), ("mxb", 0, 3, 1), ("act", 0, 2, 1), ("wq", 0, 3), ("act", 0, 3, 1), ("ld", 0, 1), ("a", 0, 2),
-    ("rg", 1, 3, "V"), ("wq", 1, 3), ("mxa", 0, 1, 3), ("ct", 0, 3), ("mxa", 0, 0, 3), ("mxa", 0, 2, 3),
-    ("act", 0, 0, 1), ("a", 0, 3), ("c02", 0, "V", 2), ("ld", 1, 1), ("c02", 0, "V", 3), ("mxa", 0, 3, 3),
-    ("rg", 1, 2, "S", 1, 4), ("rg", 0, 2, "V"), ("wq", 0, 2), ("mxb", 0, 1, 3), ("rg", 1, 2, "S", 3, 4),
-    ("xt", 0, 1, 0), ("rg", 1, 2, "S", 2, 4), ("act", 0, 1, 3), ("ld", 2, 1), ("mxb", 0, 0, 3), ("mxb", 0, 2, 3),
-    ("xcp", 0, 1, 0, "S"), ("rg", 1, 2, "S", 0, 4), ("ld", 3, 1), ("mxb", 0, 3, 3), ("xt", 0, 1, 1),
-    ("act", 0, 0, 3), ("wq", 1, 2), ("b", 0, 0, "V"), ("ct", 1, 0), ("mxa", 0, 0, 2), ("mxa", 0, 1, 2),
-    ("b", 0, 1, "V"), ("c02", 0, "V", 0), ("mxb", 0, 0, 2), ("xcp", 0, 1, 1, "S"), ("act", 0, 0, 2),
-    ("mxb", 0, 1, 2), ("xt", 1, 1, 0), ("act", 0, 2, 3), ("act", 0, 3, 3), ("tz", 0, 0), ("cnx", 0, 0),
-    ("mxa", 0, 2, 2), ("b", 0, 2, "V"), ("mxb", 0, 2, 2), ("mxa", 0, 3, 2), ("mxb", 0, 3, 2), ("tz", 0, 1),
-    ("tc", 0, 0), ("xq", 0, 1), ("xt", 1, 1, 1), ("c02", 0, "V", 1), ("to", 0, 0), ("tz", 0, 2), ("mxa", 1, 0, 0),
-    ("cnx", 0, 1), ("b", 0, 3, "V"), ("xcp", 1, 1, 0, "S"), ("tc", 0, 1), ("xcp", 1, 1, 1, "S"), ("mxa", 1, 0, 1),
-    ("act", 0, 1, 2), ("tc", 0, 2), ("xq", 1, 1), ("mxb", 1, 0, 0), ("tz", 0, 3), ("act", 0, 2, 2), ("act", 1, 0, 0),
-    ("cnx", 0, 2), ("act", 0, 3, 2), ("p8", 0, 0), ("to", 0, 1), ("mxb", 1, 0, 1), ("act", 1, 0, 1), ("hnx", 0, 0),
-    ("mxa", 1, 0, 3), ("mxb", 1, 0, 3), ("mxa", 1, 1, 0), ("cnx", 0, 3), ("mxa", 1, 1, 3), ("mxb", 1, 1, 0),
-    ("mxb", 1, 1, 3), ("mxa", 1, 0, 2), ("act", 1, 0, 3), ("to", 0, 2), ("tc", 0, 3), ("mxa", 1, 1, 1),
-    ("act", 1, 1, 3), ("mxb", 1, 1, 1), ("c02", 1, "V", 2), ("p8", 0, 1), ("hnx", 0, 1), ("mxb", 1, 0, 2),
-    ("act", 1, 1, 0), ("st", 0, "c", 0, 4), ("c02", 1, "V", 3), ("mxa", 1, 1, 2), ("act", 1, 1, 1), ("b", 1, 0, "V"),
-    ("a", 1, 0), ("mxa", 1, 2, 0), ("p8", 0, 2), ("mxb", 1, 1, 2), ("to", 0, 3), ("tz", 1, 0), ("act", 1, 0, 2),
-    ("hnx", 0, 2), ("c02", 1, "V", 0), ("to", 1, 0), ("ct", 1, 1), ("c02", 1, "V", 1), ("p8", 0, 3), ("hnx", 0, 3),
-    ("mxa", 1, 2, 2), ("mxb", 1, 2, 0), ("mxb", 1, 2, 2), ("mxa", 1, 2, 1), ("b", 1, 1, "V"), ("act", 1, 1, 2),
-    ("a", 1, 1), ("mxb", 1, 2, 1), ("tc", 1, 0), ("mxa", 1, 2, 3), ("cnx", 1, 0), ("tz", 1, 1), ("act", 1, 2, 2),
-    ("to", 1, 1), ("ct", 1, 2), ("p8", 1, 0), ("mxb", 1, 2, 3), ("act", 1, 2, 0), ("hnx", 1, 0), ("cnx", 1, 1),
-    ("tc", 1, 1), ("a", 1, 2), ("mxa", 1, 3, 3), ("mxb", 1, 3, 3), ("act", 1, 2, 1), ("mxa", 1, 3, 0),
-    ("mxa", 1, 3, 1), ("mxb", 1, 3, 1), ("p8", 1, 1), ("mxb", 1, 3, 0), ("act", 1, 2, 3), ("b", 1, 2, "V"),
-    ("tz", 1, 2), ("act", 1, 3, 3), ("ct", 1, 3), ("to", 1, 2), ("act", 1, 3, 1), ("act", 1, 3, 0), ("hnx", 1, 1),
-    ("mxa", 1, 3, 2), ("tc", 1, 2), ("b", 1, 3, "V"), ("cnx", 1, 2), ("a", 1, 3), ("st", 0, "h", 0, 4), ("p8", 1, 2),
-    ("mxb", 1, 3, 2), ("hnx", 1, 2), ("act", 1, 3, 2), ("tz", 1, 3), ("tc", 1, 3), ("to", 1, 3), ("p8", 1, 3),
-    ("st", 1, "c", 0, 3), ("st", 1, "h", 0, 3), ("cnx", 1, 3), ("hnx", 1, 3), ("st", 1, "c", 3, 4),
-    ("st", 1, "h", 3, 4),
-)
+SCALAR_PIECES = ()
+ACC = False
+GEND = True
+LAST_ON_V = True
 
 
 def tile_lstmcell_pb_kernel(tc, x, h, c, mem_read, W_ih, W_hh, bias, out_0, out_1):
@@ -69,195 +32,217 @@ def tile_lstmcell_pb_kernel(tc, x, h, c, mem_read, W_ih, W_hh, bias, out_0, out_
         inp = ctx.enter_context(tc.tile_pool(name="inp", bufs=1))
         wrawp = ctx.enter_context(tc.tile_pool(name="wraw", bufs=1))
         wgp = ctx.enter_context(tc.tile_pool(name="wg", bufs=4))
-        agp = ctx.enter_context(tc.tile_pool(name="ag", bufs=2))
+        agp = ctx.enter_context(tc.tile_pool(name="ag", bufs=4))
         codes = ctx.enter_context(tc.tile_pool(name="codes", bufs=1))
         work = ctx.enter_context(tc.tile_pool(name="work", bufs=2))
         stage = ctx.enter_context(tc.tile_pool(name="stage", bufs=2))
         psum = ctx.enter_context(tc.psum_pool(name="psum", bufs=1))
-        if PINNED:
-            ctx.enter_context(tc.manual_schedule())
 
         views = [t.rearrange("(p r) k -> p r k", r=2 * TPC) for t in (x, h, c, mem_read)]
-        outv = {"h": out_0.rearrange("(p r) k -> p r k", r=2 * TPC), "c": out_1.rearrange("(p r) k -> p r k", r=2 * TPC)}
-        weights = (W_ih, W_hh)
-        T = {}
+        names = ("x", "h", "c", "m")
+        sb = {}
 
-        def engine(e):
-            return {"V": nc.vector, "S": nc.scalar, "G": nc.gpsimd}[e]
-
-        def ld(which, n):
-            t = inp.tile([P, TPC, K], BF16, name="in%d%d" % (which, n))
+        def load_chunk(which, n):
+            t = inp.tile([P, TPC, K], BF16, name="in_%s%d" % (names[which], n))
             nc.sync.dma_start(out=t[:], in_=views[which][:, TPC * n:TPC * (n + 1), :])
-            T[("in", which, n)] = t
+            sb[(which, n)] = t
 
-        def ldW(gate, w):
-            t = wrawp.tile([P, 4, H], BF16, name="wraw%d%d" % (w, gate))
+        bz = const.tile([P, P], BF16, name="bz")
+        nc.vector.memset(bz[:], 0.0)
+        nc.scalar.dma_start(out=bz[0:16, :], in_=bias.rearrange("(t m) -> t m", m=P))
+
+        load_chunk(0, 0)
+        load_chunk(1, 0)
+        wraw = []
+        for w, wt in enumerate((W_ih, W_hh)):
+            t = wrawp.tile([P, 4, 4 * H], BF16, name="wraw%d" % w)
             for u in range(2):
                 nc.sync.dma_start(
                     out=t[:, 2 * u:2 * u + 2, :],
-                    in_=weights[w][256 * u:256 * (u + 1), H * gate:H * (gate + 1)].rearrange("(p e) c -> p e c", e=2),
+                    in_=wt[256 * u:256 * (u + 1), :].rearrange("(p e) c -> p e c", e=2),
                 )
-            T[("wraw", w, gate)] = t
+            wraw.append(t)
+        load_chunk(2, 0)
+        load_chunk(3, 0)
+        for which in range(4):
+            load_chunk(which, 1)
 
-        def setup():
-            bz = const.tile([P, P], BF16, name="bz")
-            nc.vector.memset(bz[:], 0.0)
-            nc.scalar.dma_start(out=bz[0:16, :], in_=bias.rearrange("(t m) -> t m", m=P))
-            ident_f = const.tile([P, P], F32, name="ident_f")
-            make_identity(nc, ident_f[:])
-            ident_b = const.tile([P, P], BF16, name="ident_b")
-            make_identity(nc, ident_b[:])
-            T["bz"] = bz
-            T["if"] = ident_f
-            T["ib"] = ident_b
+        ident_f = const.tile([P, P], F32, name="ident_f")
+        make_identity(nc, ident_f[:])
+        ident_b = const.tile([P, P], BF16, name="ident_b")
+        make_identity(nc, ident_b[:])
 
-        def biasT():
-            bt = psum.tile([P, P], BF16, name="bt", tag="sp")
-            nc.tensor.transpose(bt[:], T["bz"][:], T["ib"][:])
-            t = const.tile([P, 16], F32, name="biasT")
-            nc.vector.tensor_copy(out=t[:], in_=bt[:, 0:16])
-            T["bias"] = t
+        bt = psum.tile([P, P], BF16, name="bt", tag="sp")
+        nc.tensor.transpose(bt[:], bz[:], ident_b[:])
+        biasT = const.tile([P, 16], F32, name="biasT")
+        nc.vector.tensor_copy(out=biasT[:], in_=bt[:, 0:16])
 
-        def xt(o, n, q):
-            if n == 0:
-                pt = psum.tile([P, 4, P], F32, name="pt%d%d%d" % (o, n, q), tag="acc", bufs=4)
-            else:
-                pt = psum.tile([P, 4, P], F32, name="pt%d%d%d" % (o, n, q), tag="sp")
-            src32 = T[("in", o, n)][:].bitcast(F32)
+        a_codes = {}
+        a_scales = {}
+        a_grouped = {}
+
+        def act_transpose(o, n, q, tag, engine):
+            if (o, n) not in a_grouped:
+                a_grouped[(o, n)] = agp.tile([P, 4 * TPC * P], BF16, name="ag%d%d" % (o, n), tag="ag", align_bytes=64)
+            ag = a_grouped[(o, n)]
+            pt = psum.tile([P, 4, P], F32, name="pt%d%d%d" % (o, n, q), tag=tag)
+            src32 = sb[(o, n)][:].bitcast(F32)
             for rr in range(2):
                 for u in range(2):
-                    nc.tensor.transpose(pt[:, 2 * rr + u, :], src32[:, 2 * q + rr, P * u:P * (u + 1)], T["if"][:])
-            T[("pt", o, n, q)] = pt
-
-        def xcp(o, n, q, e):
-            if ("ag", o, n) not in T:
-                T[("ag", o, n)] = agp.tile([P, 4 * TPC * P], BF16, name="ag%d%d" % (o, n), tag="ag", align_bytes=64)
-            dst = T[("ag", o, n)][:].bitcast(F32)[:, 512 * q:512 * (q + 1)].rearrange("p (rr b u) -> p rr b u", rr=2, u=2)
-            src = T[("pt", o, n, q)][:].rearrange("p (rr u) b -> p rr b u", u=2)
-            if e == "V":
-                nc.vector.tensor_copy(out=dst, in_=src)
+                    nc.tensor.transpose(pt[:, 2 * rr + u, :], src32[:, 2 * q + rr, P * u:P * (u + 1)], ident_f[:])
+            dst = ag[:].bitcast(F32)[:, 512 * q:512 * (q + 1)].rearrange("p (rr b u) -> p rr b u", rr=2, u=2)
+            srcv = pt[:].rearrange("p (rr u) b -> p rr b u", u=2)
+            if engine == "v":
+                nc.vector.tensor_copy(out=dst, in_=srcv)
             else:
-                nc.scalar.copy(out=dst, in_=src)
+                nc.scalar.copy(out=dst, in_=srcv)
 
-        def xq(o, n):
+        def act_quantise(o, n):
             cd = codes.tile([P, TPC * P], U32, name="acode%d%d" % (o, n), align_bytes=64)
             sc = codes.tile([P, TPC * P], U8, name="ascale%d%d" % (o, n), align_bytes=64)
-            nc.vector.quantize_mx(out=cd[:].bitcast(FP8X4), scales=sc[:], in_=T[("ag", o, n)][:])
-            T[("ac", o, n)] = (cd, sc)
+            nc.vector.quantize_mx(out=cd[:].bitcast(FP8X4), scales=sc[:], in_=a_grouped[(o, n)][:])
+            a_codes[(o, n)] = cd
+            a_scales[(o, n)] = sc
 
-        def rg(w, gate, e, part=0, nparts=1):
-            if ("wg", w, gate) not in T:
-                T[("wg", w, gate)] = wgp.tile([P, H, 4], BF16, name="wg%d%d" % (w, gate), tag="wg", align_bytes=64)
-            width = H // nparts
-            cols = slice(width * part, width * (part + 1))
-            dst = T[("wg", w, gate)][:, cols, :].rearrange("p (cc i) t -> p cc t i", i=4)
-            src = T[("wraw", w, gate)][:, :, cols].rearrange("p t (cc i) -> p cc t i", i=4)
-            if e == "V":
-                nc.vector.tensor_copy(out=dst, in_=src)
+        act_transpose(0, 0, 0, "gf", "s")
+        act_transpose(0, 0, 1, "gi", "s")
+        act_transpose(1, 0, 0, "gg", "s")
+        act_transpose(1, 0, 1, "go", "s")
+        act_quantise(0, 0)
+        act_quantise(1, 0)
+
+        w_codes = {}
+        w_scales = {}
+
+        def weight_piece(w, j):
+            wg = wgp.tile([P, 4 * P, 4], BF16, name="wg%d%d" % (w, j), tag="wg", align_bytes=64)
+            src = wraw[w][:].rearrange("p t (g jj m) -> p t g jj m", g=4, jj=NJ)[:, :, :, j, :]
+            if (w, j) in SCALAR_PIECES:
+                nc.scalar.copy(
+                    out=wg[:].rearrange("p (g m) t -> p g m t", g=4),
+                    in_=src.rearrange("p t g m -> p g m t"),
+                )
             else:
-                nc.scalar.copy(out=dst, in_=src)
+                nc.vector.tensor_copy(
+                    out=wg[:].rearrange("p (g cc i) t -> p g cc t i", g=4, i=4),
+                    in_=src.rearrange("p t g (cc i) -> p g cc t i", i=4),
+                )
+            cd = codes.tile([P, 4 * P], U32, name="wcode%d%d" % (w, j), align_bytes=64)
+            sc = codes.tile([P, 4 * P], U8, name="wscale%d%d" % (w, j), align_bytes=64)
+            nc.vector.quantize_mx(out=cd[:].bitcast(FP8X4), scales=sc[:], in_=wg[:].rearrange("p cm t -> p (cm t)"))
+            w_codes[(w, j)] = cd
+            w_scales[(w, j)] = sc
 
-        def wq(w, gate):
-            cd = codes.tile([P, H], U32, name="wcode%d%d" % (w, gate), align_bytes=64)
-            sc = codes.tile([P, H], U8, name="wscale%d%d" % (w, gate), align_bytes=64)
-            nc.vector.quantize_mx(out=cd[:].bitcast(FP8X4), scales=sc[:], in_=T[("wg", w, gate)][:].rearrange("p cm t -> p (cm t)"))
-            T[("wc", w, gate)] = (cd, sc)
+        for j in range(NJ):
+            weight_piece(0, j)
+        for j in range(NJ):
+            weight_piece(1, j)
 
-        def mx(n, j, gate, w):
-            if w == 0:
-                T[("acc", n, j, gate)] = psum.tile([P, TPC * P], F32, name="acc", tag="acc", bufs=4)
-            wcd, wsc = T[("wc", w, gate)]
-            acd, asc = T[("ac", w, n)]
+        o0v = out_0.rearrange("(p r) k -> p r k", r=2 * TPC)
+        o1v = out_1.rearrange("(p r) k -> p r k", r=2 * TPC)
+        live = {}
+        stages = {}
+
+        def mx_pass(acc, n, j, gate, w):
             nc.tensor.matmul_mx(
-                out=T[("acc", n, j, gate)][:],
-                lhsT=wcd[:, P * j:P * (j + 1)].bitcast(FP8X4),
-                lhsT_scale=wsc[:, P * j:P * (j + 1)],
-                rhs=acd[:].bitcast(FP8X4),
-                rhs_scale=asc[:],
+                out=acc[:],
+                lhsT=w_codes[(w, j)][:, P * gate:P * (gate + 1)].bitcast(FP8X4),
+                lhsT_scale=w_scales[(w, j)][:, P * gate:P * (gate + 1)],
+                rhs=a_codes[(w, n)][:].bitcast(FP8X4),
+                rhs_scale=a_scales[(w, n)][:],
                 start=(w == 0),
                 stop=(w == 1),
             )
 
-        def mxa(n, j, gate):
-            mx(n, j, gate, 0)
-
-        def mxb(n, j, gate):
-            mx(n, j, gate, 1)
-
-        def act(n, j, gate):
-            res = work.tile([P, TPC * P], F32, name="act%d" % gate, tag="act%d" % gate, bufs=ACT_BUFS[gate])
-            col = 4 * gate + j
-            nc.scalar.activation(out=res[:], in_=T[("acc", n, j, gate)][:], func=FUNC[gate], bias=T["bias"][:, col:col + 1], scale=1.0)
-            T[("act", n, j, gate)] = res
-
-        def c02(n, e, j):
-            t = work.tile([P, TPC, P], F32, name="c02", tag="c02", bufs=4)
-            src = T[("in", 2, n)][:, :, P * j:P * (j + 1)]
-            if e == "S":
-                nc.scalar.activation(out=t[:], in_=src, func=ACT.Copy, scale=0.2)
-            else:
-                engine(e).tensor_scalar(out=t[:], in0=src, scalar1=0.2, scalar2=0.0, op0=ALU.mult, op1=ALU.add)
-            T[("c02", n, j)] = t
-
-        def ct(n, j):
-            t = psum.tile([P, TPC * P], BF16, name="ct", tag="ct")
+        def stage1(n, j):
+            acts = {}
+            order = ((GATE_F, "gf", ACT.Sigmoid), (GATE_I, "gi", ACT.Sigmoid), (GATE_G, "gg", ACT.Tanh), (GATE_O, "go", ACT.Sigmoid))
+            accs = {}
+            for gate, tag, func in order:
+                accs[gate] = psum.tile([P, TPC * P], F32, name="acc_%s" % tag, tag=tag)
+                if (n, j) == (0, 0):
+                    mx_pass(accs[gate], n, j, gate, 0)
+            for gate, tag, func in order:
+                acc = accs[gate]
+                if (n, j) != (0, 0):
+                    mx_pass(acc, n, j, gate, 0)
+                mx_pass(acc, n, j, gate, 1)
+                res = work.tile([P, TPC * P], F32, name="act_%s" % tag, tag="act_%s" % tag)
+                col = 4 * gate + j
+                nc.scalar.activation(out=res[:], in_=acc[:], func=func, bias=biasT[:, col:col + 1], scale=1.0)
+                acts[gate] = res
+            ct = psum.tile([P, TPC * P], BF16, name="ct", tag="ct")
             for s in range(TPC):
-                nc.tensor.transpose(t[:, P * s:P * (s + 1)], T[("in", 2, n)][:, s, P * j:P * (j + 1)], T["ib"][:])
-            T[("ct", n, j)] = t
+                nc.tensor.transpose(ct[:, P * s:P * (s + 1)], sb[(2, n)][:, s, P * j:P * (j + 1)], ident_b[:])
+            a8 = work.tile([P, TPC * P], F32, name="a8", tag="a8")
+            nc.vector.scalar_tensor_tensor(out=a8[:], in0=acts[GATE_F][:], scalar=0.8, in1=ct[:], op0=ALU.mult, op1=ALU.mult)
+            b8 = work.tile([P, TPC * P], F32, name="b8", tag="b8")
+            nc.vector.scalar_tensor_tensor(out=b8[:], in0=acts[GATE_I][:], scalar=0.8, in1=acts[GATE_G][:], op0=ALU.mult, op1=ALU.mult)
+            if ACC:
+                s8 = (a8, b8)
+            else:
+                s8 = work.tile([P, TPC * P], F32, name="s8", tag="s8")
+                nc.vector.tensor_tensor(out=s8[:], in0=a8[:], in1=b8[:], op=ALU.add)
+            fifth = None
+            if GEND and not (LAST_ON_V and (n, j) == (NCHUNK - 1, NJ - 1)):
+                cols = slice(P * j, P * (j + 1))
+                c02 = work.tile([P, TPC, P], F32, name="c02", tag="c02", bufs=3)
+                nc.scalar.activation(out=c02[:], in_=sb[(2, n)][:, :, cols], func=ACT.Copy, scale=0.2)
+                h02 = work.tile([P, TPC, P], F32, name="h02", tag="h02", bufs=3)
+                nc.scalar.activation(out=h02[:], in_=sb[(1, n)][:, :, cols], func=ACT.Copy, scale=0.2)
+                fifth = (c02, h02)
+            live[(n, j)] = (s8, acts[GATE_O], fifth)
 
-        def a(n, j):
-            t = work.tile([P, TPC * P], F32, name="pa", tag="pa", bufs=5)
-            nc.vector.tensor_tensor(out=t[:], in0=T[("act", n, j, GATE_F)][:], in1=T[("ct", n, j)][:], op=ALU.mult)
-            T[("pa", n, j)] = t
-
-        def b(n, j, e):
-            t = work.tile([P, TPC * P], F32, name="pb", tag="pb", bufs=2)
-            engine(e).tensor_tensor(out=t[:], in0=T[("act", n, j, GATE_I)][:], in1=T[("act", n, j, GATE_G)][:], op=ALU.mult)
-            T[("pb", n, j)] = t
-
-        def tz(n, j):
+        def stage2(n, j):
+            s8, so, fifth = live[(n, j)]
+            if j == 0:
+                hs = stage.tile([P, TPC, H], F32, name="hstage", tag="hstage")
+                cs = stage.tile([P, TPC, H], F32, name="cstage", tag="cstage")
+                stages[n] = (hs, cs)
+            hs, cs = stages[n]
+            cols = slice(P * j, P * (j + 1))
             zs = psum.tile([P, TPC, P], F32, name="zs", tag="zs")
             for s in range(TPC):
                 bcols = slice(P * s, P * (s + 1))
-                nc.tensor.matmul(zs[:, s, :], lhsT=T[("pa", n, j)][:, bcols], rhs=T["if"][:], is_transpose=True, start=True, stop=False)
-                nc.tensor.matmul(zs[:, s, :], lhsT=T[("pb", n, j)][:, bcols], rhs=T["if"][:], is_transpose=True, start=False, stop=False)
-                nc.tensor.matmul(zs[:, s, :], lhsT=T["ib"][:], rhs=T[("in", 3, n)][:, s, P * j:P * (j + 1)], start=False, stop=True)
-            T[("zs", n, j)] = zs
-
-        def tcn(n, j):
-            t = work.tile([P, TPC, P], F32, name="tcn", tag="tcn", bufs=5)
-            nc.scalar.activation(out=t[:], in_=T[("zs", n, j)][:], func=ACT.Tanh)
-            T[("tcn", n, j)] = t
-
-        def cnx(n, j):
-            if ("cst", n) not in T:
-                T[("cst", n)] = stage.tile([P, TPC, H], F32, name="cstage", tag="cstage")
-            nc.vector.scalar_tensor_tensor(out=T[("cst", n)][:, :, P * j:P * (j + 1)], in0=T[("zs", n, j)][:], scalar=0.8,
-                                           in1=T[("c02", n, j)][:], op0=ALU.mult, op1=ALU.add)
-
-        def to(n, j):
+                if ACC:
+                    nc.tensor.matmul(zs[:, s, :], lhsT=s8[0][:, bcols], rhs=ident_f[:], is_transpose=True, start=True, stop=False)
+                    nc.tensor.matmul(zs[:, s, :], lhsT=s8[1][:, bcols], rhs=ident_f[:], is_transpose=True, start=False, stop=True)
+                else:
+                    nc.tensor.transpose(zs[:, s, :], s8[:, bcols], ident_f[:])
             zo = psum.tile([P, TPC, P], F32, name="zo", tag="zo")
             for s in range(TPC):
-                nc.tensor.transpose(zo[:, s, :], T[("act", n, j, GATE_O)][:, P * s:P * (s + 1)], T["if"][:])
-            T[("zo", n, j)] = zo
+                nc.tensor.transpose(zo[:, s, :], so[:, P * s:P * (s + 1)], ident_f[:])
+            cn8 = work.tile([P, TPC, P], F32, name="cn8", tag="cn8")
+            nc.vector.scalar_tensor_tensor(out=cn8[:], in0=sb[(3, n)][:, :, cols], scalar=0.8, in1=zs[:], op0=ALU.mult, op1=ALU.add)
+            tcn = work.tile([P, TPC, P], F32, name="tcn", tag="tcn")
+            nc.scalar.activation(out=tcn[:], in_=cn8[:], func=ACT.Tanh, scale=1.25)
+            if fifth is None:
+                nc.vector.scalar_tensor_tensor(out=cs[:, :, cols], in0=sb[(2, n)][:, :, cols], scalar=0.2, in1=cn8[:], op0=ALU.mult, op1=ALU.add)
+            else:
+                nc.gpsimd.tensor_tensor(out=cs[:, :, cols], in0=fifth[0][:], in1=cn8[:], op=ALU.add)
+            p8 = work.tile([P, TPC, P], F32, name="p8", tag="p8")
+            nc.vector.scalar_tensor_tensor(out=p8[:], in0=zo[:], scalar=0.8, in1=tcn[:], op0=ALU.mult, op1=ALU.mult)
+            if fifth is None:
+                nc.vector.scalar_tensor_tensor(out=hs[:, :, cols], in0=sb[(1, n)][:, :, cols], scalar=0.2, in1=p8[:], op0=ALU.mult, op1=ALU.add)
+            else:
+                nc.gpsimd.tensor_tensor(out=hs[:, :, cols], in0=fifth[1][:], in1=p8[:], op=ALU.add)
+            rows = slice(TPC * n, TPC * (n + 1))
+            if n < NCHUNK - 1:
+                if j == NJ - 1:
+                    nc.sync.dma_start(out=o1v[:, rows, :], in_=cs[:])
+                    nc.sync.dma_start(out=o0v[:, rows, :], in_=hs[:])
+            elif j >= NJ - 2:
+                part = slice(0, P * (NJ - 1)) if j == NJ - 2 else cols
+                nc.sync.dma_start(out=o1v[:, rows, part], in_=cs[:, :, part])
+                nc.sync.dma_start(out=o0v[:, rows, part], in_=hs[:, :, part])
 
-        def p8(n, j):
-            t = work.tile([P, TPC, P], F32, name="p8", tag="p8")
-            nc.vector.scalar_tensor_tensor(out=t[:], in0=T[("zo", n, j)][:], scalar=0.8, in1=T[("tcn", n, j)][:], op0=ALU.mult, op1=ALU.mult)
-            T[("p8", n, j)] = t
-
-        def hnx(n, j):
-            if ("hst", n) not in T:
-                T[("hst", n)] = stage.tile([P, TPC, H], F32, name="hstage", tag="hstage")
-            nc.vector.scalar_tensor_tensor(out=T[("hst", n)][:, :, P * j:P * (j + 1)], in0=T[("in", 1, n)][:, :, P * j:P * (j + 1)], scalar=0.2,
-                                           in1=T[("p8", n, j)][:], op0=ALU.mult, op1=ALU.add)
-
-        def st(n, which, j0, j1):
-            cols = slice(P * j0, P * j1)
-            nc.sync.dma_start(out=outv[which][:, TPC * n:TPC * (n + 1), cols], in_=T[(which + "st", n)][:, :, cols])
-
-        ops = {"ld": ld, "ldW": ldW, "setup": setup, "biasT": biasT, "xt": xt, "xcp": xcp, "xq": xq, "rg": rg, "wq": wq,
-               "mxa": mxa, "mxb": mxb, "act": act, "c02": c02, "ct": ct, "a": a, "b": b, "tz": tz, "tc": tcn, "cnx": cnx,
-               "to": to, "p8": p8, "hnx": hnx, "st": st}
-        for step in STEPS:
-            ops[step[0]](*step[1:])
+        blocks = [(n, j) for n in range(NCHUNK) for j in range(NJ)]
+        for idx, (n, j) in enumerate(blocks):
+            stage1(n, j)
+            if idx < 4:
+                act_transpose(idx // 2, 1, idx % 2, "sp", "s")
+                if idx % 2 == 1:
+                    act_quantise(idx // 2, 1)
+            if idx > 0:
+                stage2(*blocks[idx - 1])
+        stage2(*blocks[-1])

@@ -19,10 +19,13 @@ NCHUNK = 2
 TPC = 4
 NJ = 4
 GATE_F, GATE_I, GATE_O, GATE_G = 0, 1, 2, 3
-SCALAR_PIECES = ()
-ACC = False
-GEND = True
+SCALAR_PIECES = ((0, 3), (1, 3))
+ACC = True
+GEND = False
+MEMPE = True
+C02_ENGINE = "v"
 LAST_ON_V = True
+LOAD_ORDER = (("a", 0, 0), ("a", 1, 0), ("w", 0, 0), ("w", 1, 0), ("a", 2, 0), ("a", 0, 1), ("a", 1, 1), ("w", 0, 1), ("w", 1, 1), ("a", 3, 0), ("a", 2, 1), ("a", 3, 1), ("w", 0, 2), ("w", 1, 2), ("w", 0, 3), ("w", 1, 3))
 
 
 def tile_lstmcell_pb_kernel(tc, x, h, c, mem_read, W_ih, W_hh, bias, out_0, out_1):
@@ -51,21 +54,21 @@ def tile_lstmcell_pb_kernel(tc, x, h, c, mem_read, W_ih, W_hh, bias, out_0, out_
         nc.vector.memset(bz[:], 0.0)
         nc.scalar.dma_start(out=bz[0:16, :], in_=bias.rearrange("(t m) -> t m", m=P))
 
-        load_chunk(0, 0)
-        load_chunk(1, 0)
-        wraw = []
-        for w, wt in enumerate((W_ih, W_hh)):
-            t = wrawp.tile([P, 4, 4 * H], BF16, name="wraw%d" % w)
+        wraw = {}
+
+        def load_piece(w, j):
+            t = wrawp.tile([P, 4, 4, P], BF16, name="wraw%d%d" % (w, j))
+            wt = (W_ih, W_hh)[w]
             for u in range(2):
-                nc.sync.dma_start(
-                    out=t[:, 2 * u:2 * u + 2, :],
-                    in_=wt[256 * u:256 * (u + 1), :].rearrange("(p e) c -> p e c", e=2),
-                )
-            wraw.append(t)
-        load_chunk(2, 0)
-        load_chunk(3, 0)
-        for which in range(4):
-            load_chunk(which, 1)
+                src = wt[256 * u:256 * (u + 1), :].rearrange("(p e) (g jj m) -> p e g jj m", e=2, g=4, jj=NJ)
+                nc.sync.dma_start(out=t[:, 2 * u:2 * u + 2, :, :], in_=src[:, :, :, j, :])
+            wraw[(w, j)] = t
+
+        for item in LOAD_ORDER:
+            if item[0] == "w":
+                load_piece(item[1], item[2])
+            else:
+                load_chunk(item[1], item[2])
 
         ident_f = const.tile([P, P], F32, name="ident_f")
         make_identity(nc, ident_f[:])
@@ -110,23 +113,24 @@ def tile_lstmcell_pb_kernel(tc, x, h, c, mem_read, W_ih, W_hh, bias, out_0, out_
         act_transpose(1, 0, 1, "go", "s")
         act_quantise(0, 0)
         act_quantise(1, 0)
+        act_transpose(0, 1, 0, "ct", "s")
+        act_transpose(0, 1, 1, "zs", "s")
+        act_transpose(1, 1, 0, "zo", "s")
+        act_transpose(1, 1, 1, "sp", "s")
+        act_quantise(0, 1)
+        act_quantise(1, 1)
 
         w_codes = {}
         w_scales = {}
 
         def weight_piece(w, j):
             wg = wgp.tile([P, 4 * P, 4], BF16, name="wg%d%d" % (w, j), tag="wg", align_bytes=64)
-            src = wraw[w][:].rearrange("p t (g jj m) -> p t g jj m", g=4, jj=NJ)[:, :, :, j, :]
+            dst = wg[:].rearrange("p (cc i) t -> p cc t i", i=4)
+            src = wraw[(w, j)][:].rearrange("p t g (cm i) -> p (g cm) t i", i=4)
             if (w, j) in SCALAR_PIECES:
-                nc.scalar.copy(
-                    out=wg[:].rearrange("p (g m) t -> p g m t", g=4),
-                    in_=src.rearrange("p t g m -> p g m t"),
-                )
+                nc.scalar.copy(out=dst, in_=src)
             else:
-                nc.vector.tensor_copy(
-                    out=wg[:].rearrange("p (g cc i) t -> p g cc t i", g=4, i=4),
-                    in_=src.rearrange("p t g (cc i) -> p g cc t i", i=4),
-                )
+                nc.vector.tensor_copy(out=dst, in_=src)
             cd = codes.tile([P, 4 * P], U32, name="wcode%d%d" % (w, j), align_bytes=64)
             sc = codes.tile([P, 4 * P], U8, name="wscale%d%d" % (w, j), align_bytes=64)
             nc.vector.quantize_mx(out=cd[:].bitcast(FP8X4), scales=sc[:], in_=wg[:].rearrange("p cm t -> p (cm t)"))
@@ -135,7 +139,6 @@ def tile_lstmcell_pb_kernel(tc, x, h, c, mem_read, W_ih, W_hh, bias, out_0, out_
 
         for j in range(NJ):
             weight_piece(0, j)
-        for j in range(NJ):
             weight_piece(1, j)
 
         o0v = out_0.rearrange("(p r) k -> p r k", r=2 * TPC)
@@ -175,16 +178,24 @@ def tile_lstmcell_pb_kernel(tc, x, h, c, mem_read, W_ih, W_hh, bias, out_0, out_
             for s in range(TPC):
                 nc.tensor.transpose(ct[:, P * s:P * (s + 1)], sb[(2, n)][:, s, P * j:P * (j + 1)], ident_b[:])
             a8 = work.tile([P, TPC * P], F32, name="a8", tag="a8")
-            nc.vector.scalar_tensor_tensor(out=a8[:], in0=acts[GATE_F][:], scalar=0.8, in1=ct[:], op0=ALU.mult, op1=ALU.mult)
+            nc.vector.scalar_tensor_tensor(out=a8[:], in0=acts[GATE_F][:], scalar=(1.0 if MEMPE else 0.8), in1=ct[:], op0=ALU.mult, op1=ALU.mult)
             b8 = work.tile([P, TPC * P], F32, name="b8", tag="b8")
-            nc.vector.scalar_tensor_tensor(out=b8[:], in0=acts[GATE_I][:], scalar=0.8, in1=acts[GATE_G][:], op0=ALU.mult, op1=ALU.mult)
+            nc.vector.scalar_tensor_tensor(out=b8[:], in0=acts[GATE_I][:], scalar=(1.0 if MEMPE else 0.8), in1=acts[GATE_G][:], op0=ALU.mult, op1=ALU.mult)
             if ACC:
                 s8 = (a8, b8)
             else:
                 s8 = work.tile([P, TPC * P], F32, name="s8", tag="s8")
                 nc.vector.tensor_tensor(out=s8[:], in0=a8[:], in1=b8[:], op=ALU.add)
             fifth = None
-            if GEND and not (LAST_ON_V and (n, j) == (NCHUNK - 1, NJ - 1)):
+            if MEMPE:
+                cols = slice(P * j, P * (j + 1))
+                c02 = work.tile([P, TPC, P], F32, name="c02", tag="c02", bufs=3)
+                if C02_ENGINE == "s":
+                    nc.scalar.activation(out=c02[:], in_=sb[(2, n)][:, :, cols], func=ACT.Copy, scale=0.2)
+                else:
+                    nc.vector.tensor_scalar(out=c02[:], in0=sb[(2, n)][:, :, cols], scalar1=0.2, scalar2=0.0, op0=ALU.mult, op1=ALU.add)
+                fifth = (c02, None)
+            elif GEND and not (LAST_ON_V and (n, j) == (NCHUNK - 1, NJ - 1)):
                 cols = slice(P * j, P * (j + 1))
                 c02 = work.tile([P, TPC, P], F32, name="c02", tag="c02", bufs=3)
                 nc.scalar.activation(out=c02[:], in_=sb[(2, n)][:, :, cols], func=ACT.Copy, scale=0.2)
@@ -206,43 +217,44 @@ def tile_lstmcell_pb_kernel(tc, x, h, c, mem_read, W_ih, W_hh, bias, out_0, out_
                 bcols = slice(P * s, P * (s + 1))
                 if ACC:
                     nc.tensor.matmul(zs[:, s, :], lhsT=s8[0][:, bcols], rhs=ident_f[:], is_transpose=True, start=True, stop=False)
-                    nc.tensor.matmul(zs[:, s, :], lhsT=s8[1][:, bcols], rhs=ident_f[:], is_transpose=True, start=False, stop=True)
+                    nc.tensor.matmul(zs[:, s, :], lhsT=s8[1][:, bcols], rhs=ident_f[:], is_transpose=True, start=False, stop=(not MEMPE))
+                    if MEMPE:
+                        nc.tensor.matmul(zs[:, s, :], lhsT=ident_b[:], rhs=sb[(3, n)][:, s, cols], start=False, stop=True)
                 else:
                     nc.tensor.transpose(zs[:, s, :], s8[:, bcols], ident_f[:])
             zo = psum.tile([P, TPC, P], F32, name="zo", tag="zo")
             for s in range(TPC):
                 nc.tensor.transpose(zo[:, s, :], so[:, P * s:P * (s + 1)], ident_f[:])
-            cn8 = work.tile([P, TPC, P], F32, name="cn8", tag="cn8")
-            nc.vector.scalar_tensor_tensor(out=cn8[:], in0=sb[(3, n)][:, :, cols], scalar=0.8, in1=zs[:], op0=ALU.mult, op1=ALU.add)
             tcn = work.tile([P, TPC, P], F32, name="tcn", tag="tcn")
-            nc.scalar.activation(out=tcn[:], in_=cn8[:], func=ACT.Tanh, scale=1.25)
-            if fifth is None:
+            if MEMPE:
+                nc.scalar.activation(out=tcn[:], in_=zs[:], func=ACT.Tanh)
+                nc.vector.scalar_tensor_tensor(out=cs[:, :, cols], in0=zs[:], scalar=0.8, in1=fifth[0][:], op0=ALU.mult, op1=ALU.add)
+                cn8 = None
+            else:
+                cn8 = work.tile([P, TPC, P], F32, name="cn8", tag="cn8")
+                nc.vector.scalar_tensor_tensor(out=cn8[:], in0=sb[(3, n)][:, :, cols], scalar=0.8, in1=zs[:], op0=ALU.mult, op1=ALU.add)
+                nc.scalar.activation(out=tcn[:], in_=cn8[:], func=ACT.Tanh, scale=1.25)
+            if MEMPE:
+                cn8 = None
+            elif fifth is None:
                 nc.vector.scalar_tensor_tensor(out=cs[:, :, cols], in0=sb[(2, n)][:, :, cols], scalar=0.2, in1=cn8[:], op0=ALU.mult, op1=ALU.add)
             else:
                 nc.gpsimd.tensor_tensor(out=cs[:, :, cols], in0=fifth[0][:], in1=cn8[:], op=ALU.add)
             p8 = work.tile([P, TPC, P], F32, name="p8", tag="p8")
             nc.vector.scalar_tensor_tensor(out=p8[:], in0=zo[:], scalar=0.8, in1=tcn[:], op0=ALU.mult, op1=ALU.mult)
-            if fifth is None:
+            if fifth is None or MEMPE:
                 nc.vector.scalar_tensor_tensor(out=hs[:, :, cols], in0=sb[(1, n)][:, :, cols], scalar=0.2, in1=p8[:], op0=ALU.mult, op1=ALU.add)
             else:
                 nc.gpsimd.tensor_tensor(out=hs[:, :, cols], in0=fifth[1][:], in1=p8[:], op=ALU.add)
             rows = slice(TPC * n, TPC * (n + 1))
-            if n < NCHUNK - 1:
-                if j == NJ - 1:
-                    nc.sync.dma_start(out=o1v[:, rows, :], in_=cs[:])
-                    nc.sync.dma_start(out=o0v[:, rows, :], in_=hs[:])
-            elif j >= NJ - 2:
-                part = slice(0, P * (NJ - 1)) if j == NJ - 2 else cols
+            if j >= 1:
+                part = slice(0, 2 * P) if j == 1 else cols
                 nc.sync.dma_start(out=o1v[:, rows, part], in_=cs[:, :, part])
                 nc.sync.dma_start(out=o0v[:, rows, part], in_=hs[:, :, part])
 
-        blocks = [(n, j) for n in range(NCHUNK) for j in range(NJ)]
+        blocks = [(n, j) for j in range(NJ) for n in range(NCHUNK)]
         for idx, (n, j) in enumerate(blocks):
             stage1(n, j)
-            if idx < 4:
-                act_transpose(idx // 2, 1, idx % 2, "sp", "s")
-                if idx % 2 == 1:
-                    act_quantise(idx // 2, 1)
             if idx > 0:
                 stage2(*blocks[idx - 1])
         stage2(*blocks[-1])

@@ -19,13 +19,12 @@ NCHUNK = 2
 TPC = 4
 NJ = 4
 GATE_F, GATE_I, GATE_O, GATE_G = 0, 1, 2, 3
-SCALAR_PIECES = ((0, 3), (1, 3))
-ACC = True
-GEND = False
-MEMPE = True
+GATES = ((GATE_F, "gf", ACT.Sigmoid), (GATE_I, "gi", ACT.Sigmoid), (GATE_G, "gg", ACT.Tanh), (GATE_O, "go", ACT.Sigmoid))
+X, HID, CELL, MEM = 0, 1, 2, 3
+SCALAR_PIECES = ((1, 2), (0, 3), (1, 3))
 C02_ENGINE = "v"
-LAST_ON_V = True
 LOAD_ORDER = (("a", 0, 0), ("a", 1, 0), ("w", 0, 0), ("w", 1, 0), ("a", 2, 0), ("a", 0, 1), ("a", 1, 1), ("w", 0, 1), ("w", 1, 1), ("a", 3, 0), ("a", 2, 1), ("a", 3, 1), ("w", 0, 2), ("w", 1, 2), ("w", 0, 3), ("w", 1, 3))
+BLOCKS = ((0, 0, 0, 4), (1, 0, 0, 4), (0, 1, 0, 4), (1, 1, 0, 4), (0, 2, 0, 4), (1, 2, 0, 4), (0, 3, 0, 4), (1, 3, 0, 4))
 
 
 def tile_lstmcell_pb_kernel(tc, x, h, c, mem_read, W_ih, W_hh, bias, out_0, out_1):
@@ -37,93 +36,76 @@ def tile_lstmcell_pb_kernel(tc, x, h, c, mem_read, W_ih, W_hh, bias, out_0, out_
         wgp = ctx.enter_context(tc.tile_pool(name="wg", bufs=4))
         agp = ctx.enter_context(tc.tile_pool(name="ag", bufs=4))
         codes = ctx.enter_context(tc.tile_pool(name="codes", bufs=1))
-        work = ctx.enter_context(tc.tile_pool(name="work", bufs=2))
-        stage = ctx.enter_context(tc.tile_pool(name="stage", bufs=2))
+        work = ctx.enter_context(tc.tile_pool(name="work", bufs=3))
+        stage = ctx.enter_context(tc.tile_pool(name="stage", bufs=1))
         psum = ctx.enter_context(tc.psum_pool(name="psum", bufs=1))
 
-        views = [t.rearrange("(p r) k -> p r k", r=2 * TPC) for t in (x, h, c, mem_read)]
-        names = ("x", "h", "c", "m")
+        views = [t.rearrange("(p r) k -> p r k", r=NCHUNK * TPC) for t in (x, h, c, mem_read)]
+        outs = [t.rearrange("(p r) k -> p r k", r=NCHUNK * TPC) for t in (out_0, out_1)]
         sb = {}
+        wraw = {}
 
-        def load_chunk(which, n):
-            t = inp.tile([P, TPC, K], BF16, name="in_%s%d" % (names[which], n))
+        def load_rows(which, n):
+            t = inp.tile([P, TPC, K], BF16, name="in%d%d" % (which, n))
             nc.sync.dma_start(out=t[:], in_=views[which][:, TPC * n:TPC * (n + 1), :])
             sb[(which, n)] = t
 
-        bz = const.tile([P, P], BF16, name="bz")
-        nc.vector.memset(bz[:], 0.0)
-        nc.scalar.dma_start(out=bz[0:16, :], in_=bias.rearrange("(t m) -> t m", m=P))
-
-        wraw = {}
-
-        def load_piece(w, j):
+        def load_weights(w, j):
             t = wrawp.tile([P, 4, 4, P], BF16, name="wraw%d%d" % (w, j))
-            wt = (W_ih, W_hh)[w]
             for u in range(2):
-                src = wt[256 * u:256 * (u + 1), :].rearrange("(p e) (g jj m) -> p e g jj m", e=2, g=4, jj=NJ)
+                src = (W_ih, W_hh)[w][256 * u:256 * (u + 1), :].rearrange("(p e) (g jj m) -> p e g jj m", e=2, g=4, jj=NJ)
                 nc.sync.dma_start(out=t[:, 2 * u:2 * u + 2, :, :], in_=src[:, :, :, j, :])
             wraw[(w, j)] = t
 
-        for item in LOAD_ORDER:
-            if item[0] == "w":
-                load_piece(item[1], item[2])
+        bias_rows = const.tile([P, P], BF16, name="bias_rows")
+        nc.vector.memset(bias_rows[:], 0.0)
+        nc.scalar.dma_start(out=bias_rows[0:16, :], in_=bias.rearrange("(t m) -> t m", m=P))
+        for kind, first, second in LOAD_ORDER:
+            if kind == "w":
+                load_weights(first, second)
             else:
-                load_chunk(item[1], item[2])
+                load_rows(first, second)
 
         ident_f = const.tile([P, P], F32, name="ident_f")
         make_identity(nc, ident_f[:])
         ident_b = const.tile([P, P], BF16, name="ident_b")
         make_identity(nc, ident_b[:])
 
-        bt = psum.tile([P, P], BF16, name="bt", tag="sp")
-        nc.tensor.transpose(bt[:], bz[:], ident_b[:])
-        biasT = const.tile([P, 16], F32, name="biasT")
-        nc.vector.tensor_copy(out=biasT[:], in_=bt[:, 0:16])
+        bias_t = psum.tile([P, P], BF16, name="bias_t", tag="zo")
+        nc.tensor.transpose(bias_t[:], bias_rows[:], ident_b[:])
+        bias_col = const.tile([P, 16], F32, name="bias_col")
+        nc.vector.tensor_copy(out=bias_col[:], in_=bias_t[:, 0:16])
 
         a_codes = {}
         a_scales = {}
-        a_grouped = {}
 
-        def act_transpose(o, n, q, tag, engine):
-            if (o, n) not in a_grouped:
-                a_grouped[(o, n)] = agp.tile([P, 4 * TPC * P], BF16, name="ag%d%d" % (o, n), tag="ag", align_bytes=64)
-            ag = a_grouped[(o, n)]
-            pt = psum.tile([P, 4, P], F32, name="pt%d%d%d" % (o, n, q), tag=tag)
-            src32 = sb[(o, n)][:].bitcast(F32)
-            for rr in range(2):
-                for u in range(2):
-                    nc.tensor.transpose(pt[:, 2 * rr + u, :], src32[:, 2 * q + rr, P * u:P * (u + 1)], ident_f[:])
-            dst = ag[:].bitcast(F32)[:, 512 * q:512 * (q + 1)].rearrange("p (rr b u) -> p rr b u", rr=2, u=2)
-            srcv = pt[:].rearrange("p (rr u) b -> p rr b u", u=2)
-            if engine == "v":
-                nc.vector.tensor_copy(out=dst, in_=srcv)
-            else:
-                nc.scalar.copy(out=dst, in_=srcv)
-
-        def act_quantise(o, n):
+        def quantise_rows(o, n, tags):
+            grouped = agp.tile([P, 4 * TPC * P], BF16, name="ag%d%d" % (o, n), tag="ag", align_bytes=64)
             cd = codes.tile([P, TPC * P], U32, name="acode%d%d" % (o, n), align_bytes=64)
             sc = codes.tile([P, TPC * P], U8, name="ascale%d%d" % (o, n), align_bytes=64)
-            nc.vector.quantize_mx(out=cd[:].bitcast(FP8X4), scales=sc[:], in_=a_grouped[(o, n)][:])
+            words = sb[(o, n)][:].bitcast(F32)
+            for q in range(2):
+                pt = psum.tile([P, 4, P], F32, name="pt%d%d%d" % (o, n, q), tag=tags[q], bufs=(2 if tags[q] == "zs" else 1))
+                for rr in range(2):
+                    for u in range(2):
+                        nc.tensor.transpose(pt[:, 2 * rr + u, :], words[:, 2 * q + rr, P * u:P * (u + 1)], ident_f[:])
+                dst = grouped[:].bitcast(F32)[:, 512 * q:512 * (q + 1)].rearrange("p (rr b u) -> p rr b u", rr=2, u=2)
+                nc.scalar.copy(out=dst, in_=pt[:].rearrange("p (rr u) b -> p rr b u", u=2))
+            for q in range(2):
+                half = slice(2 * P * q, 2 * P * (q + 1))
+                nc.vector.quantize_mx(out=cd[:, half].bitcast(FP8X4), scales=sc[:, half], in_=grouped[:, 8 * P * q:8 * P * (q + 1)])
             a_codes[(o, n)] = cd
             a_scales[(o, n)] = sc
 
-        act_transpose(0, 0, 0, "gf", "s")
-        act_transpose(0, 0, 1, "gi", "s")
-        act_transpose(1, 0, 0, "gg", "s")
-        act_transpose(1, 0, 1, "go", "s")
-        act_quantise(0, 0)
-        act_quantise(1, 0)
-        act_transpose(0, 1, 0, "ct", "s")
-        act_transpose(0, 1, 1, "zs", "s")
-        act_transpose(1, 1, 0, "zo", "s")
-        act_transpose(1, 1, 1, "sp", "s")
-        act_quantise(0, 1)
-        act_quantise(1, 1)
+        quantise_rows(X, 0, ("gf", "gi"))
+        quantise_rows(HID, 0, ("gg", "go"))
+        quantise_rows(X, 1, ("ct", "zs"))
+        quantise_rows(HID, 1, ("zo", "zs"))
 
         w_codes = {}
         w_scales = {}
 
-        def weight_piece(w, j):
+        def quantise_weights(w, j):
             wg = wgp.tile([P, 4 * P, 4], BF16, name="wg%d%d" % (w, j), tag="wg", align_bytes=64)
             dst = wg[:].rearrange("p (cc i) t -> p cc t i", i=4)
             src = wraw[(w, j)][:].rearrange("p t g (cm i) -> p (g cm) t i", i=4)
@@ -138,123 +120,85 @@ def tile_lstmcell_pb_kernel(tc, x, h, c, mem_read, W_ih, W_hh, bias, out_0, out_
             w_scales[(w, j)] = sc
 
         for j in range(NJ):
-            weight_piece(0, j)
-            weight_piece(1, j)
+            quantise_weights(0, j)
+            quantise_weights(1, j)
 
-        o0v = out_0.rearrange("(p r) k -> p r k", r=2 * TPC)
-        o1v = out_1.rearrange("(p r) k -> p r k", r=2 * TPC)
+        staged = {}
+        for n in range(NCHUNK):
+            staged[n] = [stage.tile([P, TPC, H], F32, name="stage%d%d" % (which, n)) for which in range(2)]
         live = {}
-        stages = {}
 
-        def mx_pass(acc, n, j, gate, w):
+        def mx_pass(acc, n, j, s0, ns, gate, w):
+            batch = slice(P * s0, P * (s0 + ns))
             nc.tensor.matmul_mx(
                 out=acc[:],
                 lhsT=w_codes[(w, j)][:, P * gate:P * (gate + 1)].bitcast(FP8X4),
                 lhsT_scale=w_scales[(w, j)][:, P * gate:P * (gate + 1)],
-                rhs=a_codes[(w, n)][:].bitcast(FP8X4),
-                rhs_scale=a_scales[(w, n)][:],
+                rhs=a_codes[(w, n)][:, batch].bitcast(FP8X4),
+                rhs_scale=a_scales[(w, n)][:, batch],
                 start=(w == 0),
                 stop=(w == 1),
             )
 
-        def stage1(n, j):
-            acts = {}
-            order = ((GATE_F, "gf", ACT.Sigmoid), (GATE_I, "gi", ACT.Sigmoid), (GATE_G, "gg", ACT.Tanh), (GATE_O, "go", ACT.Sigmoid))
-            accs = {}
-            for gate, tag, func in order:
-                accs[gate] = psum.tile([P, TPC * P], F32, name="acc_%s" % tag, tag=tag)
-                if (n, j) == (0, 0):
-                    mx_pass(accs[gate], n, j, gate, 0)
-            for gate, tag, func in order:
-                acc = accs[gate]
-                if (n, j) != (0, 0):
-                    mx_pass(acc, n, j, gate, 0)
-                mx_pass(acc, n, j, gate, 1)
-                res = work.tile([P, TPC * P], F32, name="act_%s" % tag, tag="act_%s" % tag)
-                col = 4 * gate + j
-                nc.scalar.activation(out=res[:], in_=acc[:], func=func, bias=biasT[:, col:col + 1], scale=1.0)
-                acts[gate] = res
-            ct = psum.tile([P, TPC * P], BF16, name="ct", tag="ct")
-            for s in range(TPC):
-                nc.tensor.transpose(ct[:, P * s:P * (s + 1)], sb[(2, n)][:, s, P * j:P * (j + 1)], ident_b[:])
-            a8 = work.tile([P, TPC * P], F32, name="a8", tag="a8")
-            nc.vector.scalar_tensor_tensor(out=a8[:], in0=acts[GATE_F][:], scalar=(1.0 if MEMPE else 0.8), in1=ct[:], op0=ALU.mult, op1=ALU.mult)
-            b8 = work.tile([P, TPC * P], F32, name="b8", tag="b8")
-            nc.vector.scalar_tensor_tensor(out=b8[:], in0=acts[GATE_I][:], scalar=(1.0 if MEMPE else 0.8), in1=acts[GATE_G][:], op0=ALU.mult, op1=ALU.mult)
-            if ACC:
-                s8 = (a8, b8)
-            else:
-                s8 = work.tile([P, TPC * P], F32, name="s8", tag="s8")
-                nc.vector.tensor_tensor(out=s8[:], in0=a8[:], in1=b8[:], op=ALU.add)
-            fifth = None
-            if MEMPE:
-                cols = slice(P * j, P * (j + 1))
-                c02 = work.tile([P, TPC, P], F32, name="c02", tag="c02", bufs=3)
-                if C02_ENGINE == "s":
-                    nc.scalar.activation(out=c02[:], in_=sb[(2, n)][:, :, cols], func=ACT.Copy, scale=0.2)
-                else:
-                    nc.vector.tensor_scalar(out=c02[:], in0=sb[(2, n)][:, :, cols], scalar1=0.2, scalar2=0.0, op0=ALU.mult, op1=ALU.add)
-                fifth = (c02, None)
-            elif GEND and not (LAST_ON_V and (n, j) == (NCHUNK - 1, NJ - 1)):
-                cols = slice(P * j, P * (j + 1))
-                c02 = work.tile([P, TPC, P], F32, name="c02", tag="c02", bufs=3)
-                nc.scalar.activation(out=c02[:], in_=sb[(2, n)][:, :, cols], func=ACT.Copy, scale=0.2)
-                h02 = work.tile([P, TPC, P], F32, name="h02", tag="h02", bufs=3)
-                nc.scalar.activation(out=h02[:], in_=sb[(1, n)][:, :, cols], func=ACT.Copy, scale=0.2)
-                fifth = (c02, h02)
-            live[(n, j)] = (s8, acts[GATE_O], fifth)
-
-        def stage2(n, j):
-            s8, so, fifth = live[(n, j)]
-            if j == 0:
-                hs = stage.tile([P, TPC, H], F32, name="hstage", tag="hstage")
-                cs = stage.tile([P, TPC, H], F32, name="cstage", tag="cstage")
-                stages[n] = (hs, cs)
-            hs, cs = stages[n]
+        def gates(n, j, s0, ns, x_first):
             cols = slice(P * j, P * (j + 1))
-            zs = psum.tile([P, TPC, P], F32, name="zs", tag="zs")
-            for s in range(TPC):
-                bcols = slice(P * s, P * (s + 1))
-                if ACC:
-                    nc.tensor.matmul(zs[:, s, :], lhsT=s8[0][:, bcols], rhs=ident_f[:], is_transpose=True, start=True, stop=False)
-                    nc.tensor.matmul(zs[:, s, :], lhsT=s8[1][:, bcols], rhs=ident_f[:], is_transpose=True, start=False, stop=(not MEMPE))
-                    if MEMPE:
-                        nc.tensor.matmul(zs[:, s, :], lhsT=ident_b[:], rhs=sb[(3, n)][:, s, cols], start=False, stop=True)
-                else:
-                    nc.tensor.transpose(zs[:, s, :], s8[:, bcols], ident_f[:])
-            zo = psum.tile([P, TPC, P], F32, name="zo", tag="zo")
-            for s in range(TPC):
+            rows = slice(s0, s0 + ns)
+            acts = {}
+            accs = {}
+            for gate, tag, func in GATES:
+                accs[gate] = psum.tile([P, ns * P], F32, name="acc_%s" % tag, tag=tag)
+                if x_first:
+                    mx_pass(accs[gate], n, j, s0, ns, gate, 0)
+            for gate, tag, func in GATES:
+                if not x_first:
+                    mx_pass(accs[gate], n, j, s0, ns, gate, 0)
+                mx_pass(accs[gate], n, j, s0, ns, gate, 1)
+                res = work.tile([P, ns * P], F32, name="act_%s" % tag, tag="act_%s" % tag)
+                col = 4 * gate + j
+                nc.scalar.activation(out=res[:], in_=accs[gate][:], func=func, bias=bias_col[:, col:col + 1], scale=1.0)
+                acts[gate] = res
+            ct = psum.tile([P, ns * P], BF16, name="ct", tag="ct")
+            for s in range(ns):
+                nc.tensor.transpose(ct[:, P * s:P * (s + 1)], sb[(CELL, n)][:, s0 + s, cols], ident_b[:])
+            keep = work.tile([P, ns * P], F32, name="keep", tag="keep")
+            nc.vector.tensor_tensor(out=keep[:], in0=acts[GATE_F][:], in1=ct[:], op=ALU.mult)
+            new = work.tile([P, ns * P], F32, name="new", tag="new")
+            nc.vector.tensor_tensor(out=new[:], in0=acts[GATE_I][:], in1=acts[GATE_G][:], op=ALU.mult)
+            c02 = work.tile([P, ns, P], F32, name="c02", tag="c02")
+            if C02_ENGINE == "s":
+                nc.scalar.activation(out=c02[:], in_=sb[(CELL, n)][:, rows, cols], func=ACT.Copy, scale=0.2)
+            else:
+                nc.vector.tensor_scalar(out=c02[:], in0=sb[(CELL, n)][:, rows, cols], scalar1=0.2, scalar2=0.0, op0=ALU.mult, op1=ALU.add)
+            live[(n, j, s0)] = (keep, new, acts[GATE_O], c02)
+
+        def finish(n, j, s0, ns):
+            keep, new, so, c02 = live[(n, j, s0)]
+            hs, cs = staged[n]
+            cols = slice(P * j, P * (j + 1))
+            rows = slice(s0, s0 + ns)
+            zs = psum.tile([P, ns, P], F32, name="zs", tag="zs", bufs=2)
+            nc.tensor.matmul(zs[:], lhsT=ident_b[:], rhs=sb[(MEM, n)][:, rows, cols], start=True, stop=False)
+            for s in range(ns):
+                batch = slice(P * s, P * (s + 1))
+                nc.tensor.matmul(zs[:, s, :], lhsT=keep[:, batch], rhs=ident_f[:], is_transpose=True, start=False, stop=False)
+                nc.tensor.matmul(zs[:, s, :], lhsT=new[:, batch], rhs=ident_f[:], is_transpose=True, start=False, stop=(s == ns - 1))
+            zo = psum.tile([P, ns, P], F32, name="zo", tag="zo")
+            for s in range(ns):
                 nc.tensor.transpose(zo[:, s, :], so[:, P * s:P * (s + 1)], ident_f[:])
-            tcn = work.tile([P, TPC, P], F32, name="tcn", tag="tcn")
-            if MEMPE:
-                nc.scalar.activation(out=tcn[:], in_=zs[:], func=ACT.Tanh)
-                nc.vector.scalar_tensor_tensor(out=cs[:, :, cols], in0=zs[:], scalar=0.8, in1=fifth[0][:], op0=ALU.mult, op1=ALU.add)
-                cn8 = None
-            else:
-                cn8 = work.tile([P, TPC, P], F32, name="cn8", tag="cn8")
-                nc.vector.scalar_tensor_tensor(out=cn8[:], in0=sb[(3, n)][:, :, cols], scalar=0.8, in1=zs[:], op0=ALU.mult, op1=ALU.add)
-                nc.scalar.activation(out=tcn[:], in_=cn8[:], func=ACT.Tanh, scale=1.25)
-            if MEMPE:
-                cn8 = None
-            elif fifth is None:
-                nc.vector.scalar_tensor_tensor(out=cs[:, :, cols], in0=sb[(2, n)][:, :, cols], scalar=0.2, in1=cn8[:], op0=ALU.mult, op1=ALU.add)
-            else:
-                nc.gpsimd.tensor_tensor(out=cs[:, :, cols], in0=fifth[0][:], in1=cn8[:], op=ALU.add)
-            p8 = work.tile([P, TPC, P], F32, name="p8", tag="p8")
-            nc.vector.scalar_tensor_tensor(out=p8[:], in0=zo[:], scalar=0.8, in1=tcn[:], op0=ALU.mult, op1=ALU.mult)
-            if fifth is None or MEMPE:
-                nc.vector.scalar_tensor_tensor(out=hs[:, :, cols], in0=sb[(1, n)][:, :, cols], scalar=0.2, in1=p8[:], op0=ALU.mult, op1=ALU.add)
-            else:
-                nc.gpsimd.tensor_tensor(out=hs[:, :, cols], in0=fifth[1][:], in1=p8[:], op=ALU.add)
-            rows = slice(TPC * n, TPC * (n + 1))
+            tcn = work.tile([P, ns, P], F32, name="tcn", tag="tcn")
+            nc.scalar.activation(out=tcn[:], in_=zs[:], func=ACT.Tanh)
+            nc.vector.scalar_tensor_tensor(out=cs[:, rows, cols], in0=zs[:], scalar=0.8, in1=c02[:], op0=ALU.mult, op1=ALU.add)
+            hn8 = work.tile([P, ns, P], F32, name="hn8", tag="hn8")
+            nc.vector.scalar_tensor_tensor(out=hn8[:], in0=zo[:], scalar=0.8, in1=tcn[:], op0=ALU.mult, op1=ALU.mult)
+            nc.vector.scalar_tensor_tensor(out=hs[:, rows, cols], in0=sb[(HID, n)][:, rows, cols], scalar=0.2, in1=hn8[:], op0=ALU.mult, op1=ALU.add)
             if j >= 1:
                 part = slice(0, 2 * P) if j == 1 else cols
-                nc.sync.dma_start(out=o1v[:, rows, part], in_=cs[:, :, part])
-                nc.sync.dma_start(out=o0v[:, rows, part], in_=hs[:, :, part])
+                drows = slice(TPC * n + s0, TPC * n + s0 + ns)
+                nc.sync.dma_start(out=outs[1][:, drows, part], in_=cs[:, rows, part])
+                nc.sync.dma_start(out=outs[0][:, drows, part], in_=hs[:, rows, part])
 
-        blocks = [(n, j) for j in range(NJ) for n in range(NCHUNK)]
-        for idx, (n, j) in enumerate(blocks):
-            stage1(n, j)
+        for idx, block in enumerate(BLOCKS):
+            gates(*block, idx == 0)
             if idx > 0:
-                stage2(*blocks[idx - 1])
-        stage2(*blocks[-1])
+                finish(*BLOCKS[idx - 1])
+        finish(*BLOCKS[-1])

@@ -21,7 +21,7 @@ NJ = 4
 GATE_F, GATE_I, GATE_O, GATE_G = 0, 1, 2, 3
 GATES = ((GATE_F, "gf", ACT.Sigmoid), (GATE_I, "gi", ACT.Sigmoid), (GATE_G, "gg", ACT.Tanh), (GATE_O, "go", ACT.Sigmoid))
 X, HID, CELL, MEM = 0, 1, 2, 3
-SCALAR_PIECES = ((1, 2), (0, 3), (1, 3))
+SCALAR_PIECES = ((1, 1), (1, 2), (1, 3))
 C02_ENGINE = "v"
 LOAD_ORDER = (("a", 0, 0), ("a", 1, 0), ("w", 0, 0), ("w", 1, 0), ("a", 2, 0), ("a", 0, 1), ("a", 1, 1), ("w", 0, 1), ("w", 1, 1), ("a", 3, 0), ("a", 2, 1), ("a", 3, 1), ("w", 0, 2), ("w", 1, 2), ("w", 0, 3), ("w", 1, 3))
 BLOCKS = ((0, 0, 0, 4), (1, 0, 0, 4), (0, 1, 0, 4), (1, 1, 0, 4), (0, 2, 0, 4), (1, 2, 0, 4), (0, 3, 0, 4), (1, 3, 0, 4))

@@ -23,7 +23,7 @@ GATES = ((GATE_F, "gf", ACT.Sigmoid), (GATE_I, "gi", ACT.Sigmoid), (GATE_G, "gg"
 X, HID, CELL, MEM = 0, 1, 2, 3
 SCALAR_PIECES = ((1, 1), (1, 2), (1, 3))
 C02_ENGINE = "v"
-LOAD_ORDER = (("a", 0, 0), ("a", 1, 0), ("w", 0, 0), ("w", 1, 0), ("a", 2, 0), ("a", 0, 1), ("a", 1, 1), ("w", 0, 1), ("w", 1, 1), ("a", 3, 0), ("a", 2, 1), ("a", 3, 1), ("w", 0, 2), ("w", 1, 2), ("w", 0, 3), ("w", 1, 3))
+LOAD_ORDER = (("a", 0, 0), ("a", 1, 0), ("w", 0, 0), ("w", 1, 0), ("a", 2, 0), ("a", 0, 1), ("a", 1, 1), ("a", 3, 0), ("a", 2, 1), ("w", 0, 1), ("w", 1, 1), ("a", 3, 1), ("w", 0, 2), ("w", 1, 2), ("w", 0, 3), ("w", 1, 3))
 BLOCKS = ((0, 0, 0, 4), (1, 0, 0, 4), (0, 1, 0, 4), (1, 1, 0, 4), (0, 2, 0, 4), (1, 2, 0, 4), (0, 3, 0, 4), (1, 3, 0, 4))
 
 

@@ -19,12 +19,10 @@ NCHUNK = 2
 TPC = 4
 NJ = 4
 GATE_F, GATE_I, GATE_O, GATE_G = 0, 1, 2, 3
-GATES = ((GATE_F, "gf", ACT.Sigmoid), (GATE_I, "gi", ACT.Sigmoid), (GATE_G, "gg", ACT.Tanh), (GATE_O, "go", ACT.Sigmoid))
+FUNC = {GATE_F: ACT.Sigmoid, GATE_I: ACT.Sigmoid, GATE_G: ACT.Tanh, GATE_O: ACT.Sigmoid}
+TAG = {GATE_F: "f", GATE_I: "i", GATE_G: "g", GATE_O: "o"}
+GATE_ORDER = (GATE_F, GATE_I, GATE_G, GATE_O)
 X, HID, CELL, MEM = 0, 1, 2, 3
-SCALAR_PIECES = ((1, 1), (1, 2), (1, 3))
-C02_ENGINE = "v"
-LOAD_ORDER = (("a", 0, 0), ("a", 1, 0), ("w", 0, 0), ("w", 1, 0), ("a", 2, 0), ("a", 0, 1), ("a", 1, 1), ("a", 3, 0), ("a", 2, 1), ("w", 0, 1), ("w", 1, 1), ("a", 3, 1), ("w", 0, 2), ("w", 1, 2), ("w", 0, 3), ("w", 1, 3))
-BLOCKS = ((0, 0, 0, 4), (1, 0, 0, 4), (0, 1, 0, 4), (1, 1, 0, 4), (0, 2, 0, 4), (1, 2, 0, 4), (0, 3, 0, 4), (1, 3, 0, 4))
 
 
 def tile_lstmcell_pb_kernel(tc, x, h, c, mem_read, W_ih, W_hh, bias, out_0, out_1):
@@ -39,6 +37,7 @@ def tile_lstmcell_pb_kernel(tc, x, h, c, mem_read, W_ih, W_hh, bias, out_0, out_
         work = ctx.enter_context(tc.tile_pool(name="work", bufs=3))
         stage = ctx.enter_context(tc.tile_pool(name="stage", bufs=1))
         psum = ctx.enter_context(tc.psum_pool(name="psum", bufs=1))
+        ctx.enter_context(tc.manual_schedule())
 
         views = [t.rearrange("(p r) k -> p r k", r=NCHUNK * TPC) for t in (x, h, c, mem_read)]
         outs = [t.rearrange("(p r) k -> p r k", r=NCHUNK * TPC) for t in (out_0, out_1)]
@@ -50,155 +49,241 @@ def tile_lstmcell_pb_kernel(tc, x, h, c, mem_read, W_ih, W_hh, bias, out_0, out_
             nc.sync.dma_start(out=t[:], in_=views[which][:, TPC * n:TPC * (n + 1), :])
             sb[(which, n)] = t
 
-        def load_weights(w, j):
-            t = wrawp.tile([P, 4, 4, P], BF16, name="wraw%d%d" % (w, j))
+        def load_weights(w, gate):
+            t = wrawp.tile([P, 4, H], BF16, name="wraw%d%d" % (w, gate))
             for u in range(2):
-                src = (W_ih, W_hh)[w][256 * u:256 * (u + 1), :].rearrange("(p e) (g jj m) -> p e g jj m", e=2, g=4, jj=NJ)
-                nc.sync.dma_start(out=t[:, 2 * u:2 * u + 2, :, :], in_=src[:, :, :, j, :])
-            wraw[(w, j)] = t
+                src = (W_ih, W_hh)[w][256 * u:256 * (u + 1), H * gate:H * (gate + 1)].rearrange("(p e) n -> p e n", e=2)
+                nc.sync.dma_start(out=t[:, 2 * u:2 * u + 2, :], in_=src)
+            wraw[(w, gate)] = t
+
+        warm = const.tile([P, 1], F32, name="warm")
+        nc.vector.memset(warm[:], 0.0)
+        warm_out = const.tile([P, 1], F32, name="warm_out")
+        nc.scalar.activation(out=warm_out[:], in_=warm[:], func=ACT.Sigmoid)
 
         bias_rows = const.tile([P, P], BF16, name="bias_rows")
         nc.vector.memset(bias_rows[:], 0.0)
-        nc.scalar.dma_start(out=bias_rows[0:16, :], in_=bias.rearrange("(t m) -> t m", m=P))
-        for kind, first, second in LOAD_ORDER:
-            if kind == "w":
-                load_weights(first, second)
-            else:
-                load_rows(first, second)
+        load_rows(X, 0)
+        nc.sync.dma_start(out=bias_rows[0:16, :], in_=bias.rearrange("(t m) -> t m", m=P))
+        load_rows(HID, 0)
+        load_weights(0, GATE_F)
+        load_weights(1, GATE_F)
+        load_rows(CELL, 0)
+        load_weights(0, GATE_I)
+        load_weights(1, GATE_I)
+        load_weights(0, GATE_G)
+        load_weights(1, GATE_G)
+        load_rows(MEM, 0)
+        load_weights(0, GATE_O)
+        load_weights(1, GATE_O)
+        load_rows(X, 1)
+        load_rows(HID, 1)
+        load_rows(CELL, 1)
+        load_rows(MEM, 1)
 
         ident_f = const.tile([P, P], F32, name="ident_f")
         make_identity(nc, ident_f[:])
         ident_b = const.tile([P, P], BF16, name="ident_b")
         make_identity(nc, ident_b[:])
 
-        bias_t = psum.tile([P, P], BF16, name="bias_t", tag="zo")
-        nc.tensor.transpose(bias_t[:], bias_rows[:], ident_b[:])
-        bias_col = const.tile([P, 16], F32, name="bias_col")
-        nc.vector.tensor_copy(out=bias_col[:], in_=bias_t[:, 0:16])
-
+        a_grouped = {}
         a_codes = {}
         a_scales = {}
 
-        def quantise_rows(o, n, tags):
-            grouped = agp.tile([P, 4 * TPC * P], BF16, name="ag%d%d" % (o, n), tag="ag", align_bytes=64)
-            cd = codes.tile([P, TPC * P], U32, name="acode%d%d" % (o, n), align_bytes=64)
-            sc = codes.tile([P, TPC * P], U8, name="ascale%d%d" % (o, n), align_bytes=64)
+        def turn_rows(o, n, q):
+            if q == 0:
+                a_grouped[(o, n)] = agp.tile([P, 4 * TPC * P], BF16, name="ag%d%d" % (o, n), tag="ag", align_bytes=64)
+                a_codes[(o, n)] = codes.tile([P, TPC * P], U32, name="acode%d%d" % (o, n), align_bytes=64)
+                a_scales[(o, n)] = codes.tile([P, TPC * P], U8, name="ascale%d%d" % (o, n), align_bytes=64)
             words = sb[(o, n)][:].bitcast(F32)
-            for q in range(2):
-                pt = psum.tile([P, 4, P], F32, name="pt%d%d%d" % (o, n, q), tag=tags[q], bufs=(2 if tags[q] == "zs" else 1))
-                for rr in range(2):
-                    for u in range(2):
-                        nc.tensor.transpose(pt[:, 2 * rr + u, :], words[:, 2 * q + rr, P * u:P * (u + 1)], ident_f[:])
-                dst = grouped[:].bitcast(F32)[:, 512 * q:512 * (q + 1)].rearrange("p (rr b u) -> p rr b u", rr=2, u=2)
-                nc.scalar.copy(out=dst, in_=pt[:].rearrange("p (rr u) b -> p rr b u", u=2))
-            for q in range(2):
-                half = slice(2 * P * q, 2 * P * (q + 1))
-                nc.vector.quantize_mx(out=cd[:, half].bitcast(FP8X4), scales=sc[:, half], in_=grouped[:, 8 * P * q:8 * P * (q + 1)])
-            a_codes[(o, n)] = cd
-            a_scales[(o, n)] = sc
+            pt = psum.tile([P, 4, P], F32, name="acc", tag="acc", bufs=3)
+            for rr in range(2):
+                for u in range(2):
+                    nc.tensor.transpose(pt[:, 2 * rr + u, :], words[:, 2 * q + rr, P * u:P * (u + 1)], ident_f[:])
+            dst = a_grouped[(o, n)][:].bitcast(F32)[:, 512 * q:512 * (q + 1)].rearrange("p (rr b u) -> p rr b u", rr=2, u=2)
+            nc.scalar.copy(out=dst, in_=pt[:].rearrange("p (rr u) b -> p rr b u", u=2))
 
-        quantise_rows(X, 0, ("gf", "gi"))
-        quantise_rows(HID, 0, ("gg", "go"))
-        quantise_rows(X, 1, ("ct", "zs"))
-        quantise_rows(HID, 1, ("zo", "zs"))
+        def quantise_rows(o, n, q):
+            half = slice(2 * P * q, 2 * P * (q + 1))
+            nc.vector.quantize_mx(out=a_codes[(o, n)][:, half].bitcast(FP8X4), scales=a_scales[(o, n)][:, half], in_=a_grouped[(o, n)][:, 8 * P * q:8 * P * (q + 1)])
 
+        w_grouped = {}
         w_codes = {}
         w_scales = {}
 
-        def quantise_weights(w, j):
-            wg = wgp.tile([P, 4 * P, 4], BF16, name="wg%d%d" % (w, j), tag="wg", align_bytes=64)
-            dst = wg[:].rearrange("p (cc i) t -> p cc t i", i=4)
-            src = wraw[(w, j)][:].rearrange("p t g (cm i) -> p (g cm) t i", i=4)
-            if (w, j) in SCALAR_PIECES:
+        def regroup(w, j, half, engine):
+            if (w, j) not in w_grouped:
+                w_grouped[(w, j)] = wgp.tile([P, 4 * P, 4], BF16, name="wg%d%d" % (w, j), tag="wg", align_bytes=64)
+                w_codes[(w, j)] = codes.tile([P, 4 * P], U32, name="wcode%d%d" % (w, j), align_bytes=64)
+                w_scales[(w, j)] = codes.tile([P, 4 * P], U8, name="wscale%d%d" % (w, j), align_bytes=64)
+            cols = slice(0, 4 * P) if half is None else slice(2 * P * half, 2 * P * (half + 1))
+            dst = w_grouped[(w, j)][:, cols, :].rearrange("p (cc i) t -> p cc t i", i=4)
+            src = wraw[(w, j)][:, :, cols].rearrange("p t (cm i) -> p cm t i", i=4)
+            if engine == "s":
                 nc.scalar.copy(out=dst, in_=src)
             else:
                 nc.vector.tensor_copy(out=dst, in_=src)
-            cd = codes.tile([P, 4 * P], U32, name="wcode%d%d" % (w, j), align_bytes=64)
-            sc = codes.tile([P, 4 * P], U8, name="wscale%d%d" % (w, j), align_bytes=64)
-            nc.vector.quantize_mx(out=cd[:].bitcast(FP8X4), scales=sc[:], in_=wg[:].rearrange("p cm t -> p (cm t)"))
-            w_codes[(w, j)] = cd
-            w_scales[(w, j)] = sc
 
-        for j in range(NJ):
-            quantise_weights(0, j)
-            quantise_weights(1, j)
+        def quantise_weights(w, j, half=None):
+            cols = slice(0, 4 * P) if half is None else slice(2 * P * half, 2 * P * (half + 1))
+            nc.vector.quantize_mx(out=w_codes[(w, j)][:, cols].bitcast(FP8X4), scales=w_scales[(w, j)][:, cols], in_=w_grouped[(w, j)][:, cols, :].rearrange("p cm t -> p (cm t)"))
 
         staged = {}
         for n in range(NCHUNK):
             staged[n] = [stage.tile([P, TPC, H], F32, name="stage%d%d" % (which, n)) for which in range(2)]
-        live = {}
+        accs = {}
+        acts = {}
+        cts = {}
+        kept = {}
+        news = {}
+        c02s = {}
+        zss = {}
+        zos = {}
 
-        def mx_pass(acc, n, j, s0, ns, gate, w):
-            batch = slice(P * s0, P * (s0 + ns))
+        def mx_pass(n, j, gate, w):
+            if w == 0:
+                accs[(n, j, gate)] = psum.tile([P, TPC * P], F32, name="acc", tag="acc", bufs=3)
             nc.tensor.matmul_mx(
-                out=acc[:],
-                lhsT=w_codes[(w, j)][:, P * gate:P * (gate + 1)].bitcast(FP8X4),
-                lhsT_scale=w_scales[(w, j)][:, P * gate:P * (gate + 1)],
-                rhs=a_codes[(w, n)][:, batch].bitcast(FP8X4),
-                rhs_scale=a_scales[(w, n)][:, batch],
+                out=accs[(n, j, gate)][:],
+                lhsT=w_codes[(w, gate)][:, P * j:P * (j + 1)].bitcast(FP8X4),
+                lhsT_scale=w_scales[(w, gate)][:, P * j:P * (j + 1)],
+                rhs=a_codes[(w, n)][:].bitcast(FP8X4),
+                rhs_scale=a_scales[(w, n)][:],
                 start=(w == 0),
                 stop=(w == 1),
             )
 
-        def gates(n, j, s0, ns, x_first):
-            cols = slice(P * j, P * (j + 1))
-            rows = slice(s0, s0 + ns)
-            acts = {}
-            accs = {}
-            for gate, tag, func in GATES:
-                accs[gate] = psum.tile([P, ns * P], F32, name="acc_%s" % tag, tag=tag)
-                if x_first:
-                    mx_pass(accs[gate], n, j, s0, ns, gate, 0)
-            for gate, tag, func in GATES:
-                if not x_first:
-                    mx_pass(accs[gate], n, j, s0, ns, gate, 0)
-                mx_pass(accs[gate], n, j, s0, ns, gate, 1)
-                res = work.tile([P, ns * P], F32, name="act_%s" % tag, tag="act_%s" % tag)
-                col = 4 * gate + j
-                nc.scalar.activation(out=res[:], in_=accs[gate][:], func=func, bias=bias_col[:, col:col + 1], scale=1.0)
-                acts[gate] = res
-            ct = psum.tile([P, ns * P], BF16, name="ct", tag="ct")
-            for s in range(ns):
-                nc.tensor.transpose(ct[:, P * s:P * (s + 1)], sb[(CELL, n)][:, s0 + s, cols], ident_b[:])
-            keep = work.tile([P, ns * P], F32, name="keep", tag="keep")
-            nc.vector.tensor_tensor(out=keep[:], in0=acts[GATE_F][:], in1=ct[:], op=ALU.mult)
-            new = work.tile([P, ns * P], F32, name="new", tag="new")
-            nc.vector.tensor_tensor(out=new[:], in0=acts[GATE_I][:], in1=acts[GATE_G][:], op=ALU.mult)
-            c02 = work.tile([P, ns, P], F32, name="c02", tag="c02")
-            if C02_ENGINE == "s":
-                nc.scalar.activation(out=c02[:], in_=sb[(CELL, n)][:, rows, cols], func=ACT.Copy, scale=0.2)
-            else:
-                nc.vector.tensor_scalar(out=c02[:], in0=sb[(CELL, n)][:, rows, cols], scalar1=0.2, scalar2=0.0, op0=ALU.mult, op1=ALU.add)
-            live[(n, j, s0)] = (keep, new, acts[GATE_O], c02)
+        def gate_act(n, j, gate):
+            res = work.tile([P, TPC * P], F32, name="act_%s" % TAG[gate], tag="act_%s" % TAG[gate], bufs=5)
+            col = 4 * gate + j
+            nc.scalar.activation(out=res[:], in_=accs[(n, j, gate)][:], func=FUNC[gate], bias=bias_col[:, col:col + 1], scale=1.0)
+            acts[(n, j, gate)] = res
 
-        def finish(n, j, s0, ns):
-            keep, new, so, c02 = live[(n, j, s0)]
+        def turn_cells(n, first):
+            ct = psum.tile([P, 2, TPC * P], BF16, name="ct", tag="ct")
+            for i in range(2):
+                for s in range(TPC):
+                    nc.tensor.transpose(ct[:, i, P * s:P * (s + 1)], sb[(CELL, n)][:, s, P * (first + i):P * (first + i + 1)], ident_b[:])
+                cts[(n, first + i)] = ct[:, i, :]
+
+        def keep(n, j):
+            t = work.tile([P, TPC * P], F32, name="keep", tag="keep", bufs=5)
+            nc.vector.tensor_tensor(out=t[:], in0=acts[(n, j, GATE_F)][:], in1=cts[(n, j)], op=ALU.mult)
+            kept[(n, j)] = t
+
+        def new(n, j):
+            t = work.tile([P, TPC * P], F32, name="new", tag="new", bufs=5)
+            nc.vector.tensor_tensor(out=t[:], in0=acts[(n, j, GATE_I)][:], in1=acts[(n, j, GATE_G)][:], op=ALU.mult)
+            news[(n, j)] = t
+
+        def fifth_of_cell(n, j):
+            t = work.tile([P, TPC, P], F32, name="c02", tag="c02")
+            nc.scalar.activation(out=t[:], in_=sb[(CELL, n)][:, :, P * j:P * (j + 1)], func=ACT.Copy, scale=0.2)
+            c02s[(n, j)] = t
+
+        def sums(n, j):
+            zs = psum.tile([P, TPC, P], F32, name="zs", tag="zs", bufs=2)
+            nc.tensor.matmul(zs[:], lhsT=ident_b[:], rhs=sb[(MEM, n)][:, :, P * j:P * (j + 1)], start=True, stop=False)
+            for s in range(TPC):
+                batch = slice(P * s, P * (s + 1))
+                nc.tensor.matmul(zs[:, s, :], lhsT=kept[(n, j)][:, batch], rhs=ident_f[:], is_transpose=True, start=False, stop=False)
+                nc.tensor.matmul(zs[:, s, :], lhsT=news[(n, j)][:, batch], rhs=ident_f[:], is_transpose=True, start=False, stop=(s == TPC - 1))
+            zss[(n, j)] = zs
+
+        def turn_output_gate(n, j):
+            zo = psum.tile([P, TPC, P], F32, name="zo", tag="zo", bufs=2)
+            for s in range(TPC):
+                nc.tensor.transpose(zo[:, s, :], acts[(n, j, GATE_O)][:, P * s:P * (s + 1)], ident_f[:])
+            zos[(n, j)] = zo
+
+        tcns = {}
+
+        def tanh_cell(n, j):
+            t = work.tile([P, TPC, P], F32, name="tcn", tag="tcn")
+            nc.scalar.activation(out=t[:], in_=zss[(n, j)][:], func=ACT.Tanh)
+            tcns[(n, j)] = t
+
+        def outputs(n, j):
             hs, cs = staged[n]
             cols = slice(P * j, P * (j + 1))
-            rows = slice(s0, s0 + ns)
-            zs = psum.tile([P, ns, P], F32, name="zs", tag="zs", bufs=2)
-            nc.tensor.matmul(zs[:], lhsT=ident_b[:], rhs=sb[(MEM, n)][:, rows, cols], start=True, stop=False)
-            for s in range(ns):
-                batch = slice(P * s, P * (s + 1))
-                nc.tensor.matmul(zs[:, s, :], lhsT=keep[:, batch], rhs=ident_f[:], is_transpose=True, start=False, stop=False)
-                nc.tensor.matmul(zs[:, s, :], lhsT=new[:, batch], rhs=ident_f[:], is_transpose=True, start=False, stop=(s == ns - 1))
-            zo = psum.tile([P, ns, P], F32, name="zo", tag="zo")
-            for s in range(ns):
-                nc.tensor.transpose(zo[:, s, :], so[:, P * s:P * (s + 1)], ident_f[:])
-            tcn = work.tile([P, ns, P], F32, name="tcn", tag="tcn")
-            nc.scalar.activation(out=tcn[:], in_=zs[:], func=ACT.Tanh)
-            nc.vector.scalar_tensor_tensor(out=cs[:, rows, cols], in0=zs[:], scalar=0.8, in1=c02[:], op0=ALU.mult, op1=ALU.add)
-            hn8 = work.tile([P, ns, P], F32, name="hn8", tag="hn8")
-            nc.vector.scalar_tensor_tensor(out=hn8[:], in0=zo[:], scalar=0.8, in1=tcn[:], op0=ALU.mult, op1=ALU.mult)
-            nc.vector.scalar_tensor_tensor(out=hs[:, rows, cols], in0=sb[(HID, n)][:, rows, cols], scalar=0.2, in1=hn8[:], op0=ALU.mult, op1=ALU.add)
+            nc.vector.scalar_tensor_tensor(out=cs[:, :, cols], in0=zss[(n, j)][:], scalar=0.8, in1=c02s[(n, j)][:], op0=ALU.mult, op1=ALU.add)
+            hn8 = work.tile([P, TPC, P], F32, name="hn8", tag="hn8")
+            nc.vector.scalar_tensor_tensor(out=hn8[:], in0=zos[(n, j)][:], scalar=0.8, in1=tcns[(n, j)][:], op0=ALU.mult, op1=ALU.mult)
+            nc.vector.scalar_tensor_tensor(out=hs[:, :, cols], in0=sb[(HID, n)][:, :, cols], scalar=0.2, in1=hn8[:], op0=ALU.mult, op1=ALU.add)
             if j >= 1:
                 part = slice(0, 2 * P) if j == 1 else cols
-                drows = slice(TPC * n + s0, TPC * n + s0 + ns)
-                nc.sync.dma_start(out=outs[1][:, drows, part], in_=cs[:, rows, part])
-                nc.sync.dma_start(out=outs[0][:, drows, part], in_=hs[:, rows, part])
+                rows = slice(TPC * n, TPC * (n + 1))
+                nc.sync.dma_start(out=outs[1][:, rows, part], in_=cs[:, :, part])
+                nc.sync.dma_start(out=outs[0][:, rows, part], in_=hs[:, :, part])
 
-        for idx, block in enumerate(BLOCKS):
-            gates(*block, idx == 0)
-            if idx > 0:
-                finish(*BLOCKS[idx - 1])
-        finish(*BLOCKS[-1])
+        for q in range(2):
+            turn_rows(X, 0, q)
+        for q in range(2):
+            turn_rows(HID, 0, q)
+        bias_t = psum.tile([P, P], BF16, name="bias_t", tag="ct")
+        nc.tensor.transpose(bias_t[:], bias_rows[:], ident_b[:])
+        for q in range(2):
+            quantise_rows(X, 0, q)
+        for q in range(2):
+            quantise_rows(HID, 0, q)
+        bias_col = const.tile([P, 16], F32, name="bias_col")
+        nc.vector.tensor_copy(out=bias_col[:], in_=bias_t[:, 0:16])
+
+        for g, gate in enumerate(GATE_ORDER):
+            regroup(0, gate, None, "v")
+            regroup(1, gate, 1, "s")
+            regroup(1, gate, 0, "v")
+            quantise_weights(0, gate)
+            quantise_weights(1, gate, 0)
+            for j in {1: (0, 1), 2: (2, 3)}.get(g, ()):
+                keep(0, j)
+            if g == 3:
+                new(0, 0)
+                new(0, 1)
+            quantise_weights(1, gate, 1)
+            for j in range(NJ):
+                for w in range(2):
+                    mx_pass(0, j, gate, w)
+            if g < 2:
+                turn_cells(0, 2 * g)
+            for j in range(NJ):
+                gate_act(0, j, gate)
+            if g == 2:
+                fifth_of_cell(0, 0)
+        for j in (2, 3):
+            new(0, j)
+        for o in (X, HID):
+            for q in range(2):
+                turn_rows(o, 1, q)
+        sums(0, 0)
+        turn_output_gate(0, 0)
+        for o in (X, HID):
+            for q in range(2):
+                quantise_rows(o, 1, q)
+        tanh_cell(0, 0)
+
+        UNITS = ((0, 0), (0, 1), (1, 0), (0, 2), (1, 1), (0, 3), (1, 2), (1, 3))
+
+        def stage_one(n, j):
+            sums(n, j)
+            turn_output_gate(n, j)
+            tanh_cell(n, j)
+
+        fifth_of_cell(*UNITS[1])
+        for j in range(NJ):
+            if j % 2 == 0:
+                turn_cells(1, j)
+            for gate in GATE_ORDER:
+                mx_pass(1, j, gate, 0)
+                mx_pass(1, j, gate, 1)
+                gate_act(1, j, gate)
+            outputs(*UNITS[2 * j])
+            keep(1, j)
+            new(1, j)
+            for u in (2 * j + 1, 2 * j + 2):
+                if u < 8:
+                    stage_one(*UNITS[u])
+                    if u + 1 < 8:
+                        fifth_of_cell(*UNITS[u + 1])
+                    if u % 2:
+                        outputs(*UNITS[u])

@@ -20,7 +20,7 @@ TPC = 4
 NJ = 4
 GATE_F, GATE_I, GATE_O, GATE_G = 0, 1, 2, 3
 FUNC = {GATE_F: ACT.Sigmoid, GATE_I: ACT.Sigmoid, GATE_G: ACT.Tanh, GATE_O: ACT.Sigmoid}
-TAG = {GATE_F: "f", GATE_I: "i", GATE_G: "g", GATE_O: "o"}
+TAG = {GATE_F: "gf", GATE_I: "gi", GATE_G: "gg", GATE_O: "go"}
 GATE_ORDER = (GATE_F, GATE_I, GATE_G, GATE_O)
 X, HID, CELL, MEM = 0, 1, 2, 3
 
@@ -49,12 +49,14 @@ def tile_lstmcell_pb_kernel(tc, x, h, c, mem_read, W_ih, W_hh, bias, out_0, out_
             nc.sync.dma_start(out=t[:], in_=views[which][:, TPC * n:TPC * (n + 1), :])
             sb[(which, n)] = t
 
-        def load_weights(w, gate):
-            t = wrawp.tile([P, 4, H], BF16, name="wraw%d%d" % (w, gate))
-            for u in range(2):
-                src = (W_ih, W_hh)[w][256 * u:256 * (u + 1), H * gate:H * (gate + 1)].rearrange("(p e) n -> p e n", e=2)
-                nc.sync.dma_start(out=t[:, 2 * u:2 * u + 2, :], in_=src)
-            wraw[(w, gate)] = t
+        def load_weights(gate, half):
+            t = wrawp.tile([P, 4, 2, 2 * P], BF16, name="wraw%d%d" % (gate, half))
+            first = H * gate + 2 * P * half
+            for w in range(2):
+                for u in range(2):
+                    src = (W_ih, W_hh)[w][256 * u:256 * (u + 1), first:first + 2 * P].rearrange("(p e) n -> p e n", e=2)
+                    nc.sync.dma_start(out=t[:, 2 * u:2 * u + 2, w, :], in_=src)
+            wraw[(gate, half)] = t
 
         warm = const.tile([P, 1], F32, name="warm")
         nc.vector.memset(warm[:], 0.0)
@@ -63,23 +65,21 @@ def tile_lstmcell_pb_kernel(tc, x, h, c, mem_read, W_ih, W_hh, bias, out_0, out_
 
         bias_rows = const.tile([P, P], BF16, name="bias_rows")
         nc.vector.memset(bias_rows[:], 0.0)
+        load_weights(GATE_F, 0)
         load_rows(X, 0)
         nc.sync.dma_start(out=bias_rows[0:16, :], in_=bias.rearrange("(t m) -> t m", m=P))
         load_rows(HID, 0)
-        load_weights(0, GATE_F)
-        load_weights(1, GATE_F)
+        load_weights(GATE_I, 0)
+        load_weights(GATE_G, 0)
         load_rows(CELL, 0)
-        load_weights(0, GATE_I)
-        load_weights(1, GATE_I)
-        load_weights(0, GATE_G)
-        load_weights(1, GATE_G)
-        load_rows(MEM, 0)
-        load_weights(0, GATE_O)
-        load_weights(1, GATE_O)
         load_rows(X, 1)
         load_rows(HID, 1)
+        load_weights(GATE_O, 0)
         load_rows(CELL, 1)
+        load_rows(MEM, 0)
         load_rows(MEM, 1)
+        for gate in GATE_ORDER:
+            load_weights(gate, 1)
 
         ident_f = const.tile([P, P], F32, name="ident_f")
         make_identity(nc, ident_f[:])
@@ -111,22 +111,19 @@ def tile_lstmcell_pb_kernel(tc, x, h, c, mem_read, W_ih, W_hh, bias, out_0, out_
         w_codes = {}
         w_scales = {}
 
-        def regroup(w, j, half, engine):
-            if (w, j) not in w_grouped:
-                w_grouped[(w, j)] = wgp.tile([P, 4 * P, 4], BF16, name="wg%d%d" % (w, j), tag="wg", align_bytes=64)
-                w_codes[(w, j)] = codes.tile([P, 4 * P], U32, name="wcode%d%d" % (w, j), align_bytes=64)
-                w_scales[(w, j)] = codes.tile([P, 4 * P], U8, name="wscale%d%d" % (w, j), align_bytes=64)
-            cols = slice(0, 4 * P) if half is None else slice(2 * P * half, 2 * P * (half + 1))
-            dst = w_grouped[(w, j)][:, cols, :].rearrange("p (cc i) t -> p cc t i", i=4)
-            src = wraw[(w, j)][:, :, cols].rearrange("p t (cm i) -> p cm t i", i=4)
+        def regroup(gate, half, engine):
+            w_grouped[(gate, half)] = wgp.tile([P, 4 * P, 4], BF16, name="wg%d%d" % (gate, half), tag="wg", align_bytes=64)
+            w_codes[(gate, half)] = codes.tile([P, 4 * P], U32, name="wcode%d%d" % (gate, half), align_bytes=64)
+            w_scales[(gate, half)] = codes.tile([P, 4 * P], U8, name="wscale%d%d" % (gate, half), align_bytes=64)
+            dst = w_grouped[(gate, half)][:].rearrange("p (cc i) t -> p cc t i", i=4)
+            src = wraw[(gate, half)][:].rearrange("p t w (cm i) -> p (w cm) t i", i=4)
             if engine == "s":
                 nc.scalar.copy(out=dst, in_=src)
             else:
                 nc.vector.tensor_copy(out=dst, in_=src)
 
-        def quantise_weights(w, j, half=None):
-            cols = slice(0, 4 * P) if half is None else slice(2 * P * half, 2 * P * (half + 1))
-            nc.vector.quantize_mx(out=w_codes[(w, j)][:, cols].bitcast(FP8X4), scales=w_scales[(w, j)][:, cols], in_=w_grouped[(w, j)][:, cols, :].rearrange("p cm t -> p (cm t)"))
+        def quantise_weights(gate, half):
+            nc.vector.quantize_mx(out=w_codes[(gate, half)][:].bitcast(FP8X4), scales=w_scales[(gate, half)][:], in_=w_grouped[(gate, half)][:].rearrange("p cm t -> p (cm t)"))
 
         staged = {}
         for n in range(NCHUNK):
@@ -139,14 +136,17 @@ def tile_lstmcell_pb_kernel(tc, x, h, c, mem_read, W_ih, W_hh, bias, out_0, out_
         c02s = {}
         zss = {}
         zos = {}
+        tcns = {}
+        hn8s = {}
 
         def mx_pass(n, j, gate, w):
+            cols = slice(P * (2 * w + j % 2), P * (2 * w + j % 2 + 1))
             if w == 0:
                 accs[(n, j, gate)] = psum.tile([P, TPC * P], F32, name="acc", tag="acc", bufs=3)
             nc.tensor.matmul_mx(
                 out=accs[(n, j, gate)][:],
-                lhsT=w_codes[(w, gate)][:, P * j:P * (j + 1)].bitcast(FP8X4),
-                lhsT_scale=w_scales[(w, gate)][:, P * j:P * (j + 1)],
+                lhsT=w_codes[(gate, j // 2)][:, cols].bitcast(FP8X4),
+                lhsT_scale=w_scales[(gate, j // 2)][:, cols],
                 rhs=a_codes[(w, n)][:].bitcast(FP8X4),
                 rhs_scale=a_scales[(w, n)][:],
                 start=(w == 0),
@@ -154,136 +154,201 @@ def tile_lstmcell_pb_kernel(tc, x, h, c, mem_read, W_ih, W_hh, bias, out_0, out_
             )
 
         def gate_act(n, j, gate):
-            res = work.tile([P, TPC * P], F32, name="act_%s" % TAG[gate], tag="act_%s" % TAG[gate], bufs=5)
+            if j % 2 == 0:
+                acts[(n, j // 2, gate)] = work.tile([P, 2, TPC * P], F32, name="act_%s" % TAG[gate], tag="act_%s" % TAG[gate], bufs=2)
             col = 4 * gate + j
-            nc.scalar.activation(out=res[:], in_=accs[(n, j, gate)][:], func=FUNC[gate], bias=bias_col[:, col:col + 1], scale=1.0)
-            acts[(n, j, gate)] = res
+            nc.scalar.activation(out=acts[(n, j // 2, gate)][:, j % 2, :], in_=accs[(n, j, gate)][:], func=FUNC[gate], bias=bias_col[:, col:col + 1], scale=1.0)
 
-        def turn_cells(n, first):
+        def turn_cells(n, half):
             ct = psum.tile([P, 2, TPC * P], BF16, name="ct", tag="ct")
             for i in range(2):
                 for s in range(TPC):
-                    nc.tensor.transpose(ct[:, i, P * s:P * (s + 1)], sb[(CELL, n)][:, s, P * (first + i):P * (first + i + 1)], ident_b[:])
-                cts[(n, first + i)] = ct[:, i, :]
+                    nc.tensor.transpose(ct[:, i, P * s:P * (s + 1)], sb[(CELL, n)][:, s, P * (2 * half + i):P * (2 * half + i + 1)], ident_b[:])
+            cts[(n, half)] = ct
 
-        def keep(n, j):
-            t = work.tile([P, TPC * P], F32, name="keep", tag="keep", bufs=5)
-            nc.vector.tensor_tensor(out=t[:], in0=acts[(n, j, GATE_F)][:], in1=cts[(n, j)], op=ALU.mult)
-            kept[(n, j)] = t
+        def keep(n, half, i=None):
+            which = slice(0, 2) if i is None else slice(i, i + 1)
+            if not i:
+                kept[(n, half)] = work.tile([P, 2, TPC * P], F32, name="keep", tag="keep", bufs=2)
+            nc.vector.tensor_tensor(out=kept[(n, half)][:, which, :], in0=acts[(n, half, GATE_F)][:, which, :], in1=cts[(n, half)][:, which, :], op=ALU.mult)
 
-        def new(n, j):
-            t = work.tile([P, TPC * P], F32, name="new", tag="new", bufs=5)
-            nc.vector.tensor_tensor(out=t[:], in0=acts[(n, j, GATE_I)][:], in1=acts[(n, j, GATE_G)][:], op=ALU.mult)
-            news[(n, j)] = t
+        def new(n, half, i=None):
+            which = slice(0, 2) if i is None else slice(i, i + 1)
+            if not i:
+                news[(n, half)] = work.tile([P, 2, TPC * P], F32, name="new", tag="new", bufs=2)
+            nc.vector.tensor_tensor(out=news[(n, half)][:, which, :], in0=acts[(n, half, GATE_I)][:, which, :], in1=acts[(n, half, GATE_G)][:, which, :], op=ALU.mult)
 
-        def fifth_of_cell(n, j):
-            t = work.tile([P, TPC, P], F32, name="c02", tag="c02")
-            nc.scalar.activation(out=t[:], in_=sb[(CELL, n)][:, :, P * j:P * (j + 1)], func=ACT.Copy, scale=0.2)
-            c02s[(n, j)] = t
+        def fifth_of_cell(n, half, engine):
+            t = work.tile([P, TPC, 2 * P], F32, name="c02", tag="c02", bufs=3)
+            src = sb[(CELL, n)][:, :, 2 * P * half:2 * P * (half + 1)]
+            if engine == "s":
+                nc.scalar.activation(out=t[:], in_=src, func=ACT.Copy, scale=0.2)
+            else:
+                nc.vector.tensor_scalar(out=t[:], in0=src, scalar1=0.2, scalar2=0.0, op0=ALU.mult, op1=ALU.add)
+            c02s[(n, half)] = t
 
         def sums(n, j):
             zs = psum.tile([P, TPC, P], F32, name="zs", tag="zs", bufs=2)
             nc.tensor.matmul(zs[:], lhsT=ident_b[:], rhs=sb[(MEM, n)][:, :, P * j:P * (j + 1)], start=True, stop=False)
             for s in range(TPC):
                 batch = slice(P * s, P * (s + 1))
-                nc.tensor.matmul(zs[:, s, :], lhsT=kept[(n, j)][:, batch], rhs=ident_f[:], is_transpose=True, start=False, stop=False)
-                nc.tensor.matmul(zs[:, s, :], lhsT=news[(n, j)][:, batch], rhs=ident_f[:], is_transpose=True, start=False, stop=(s == TPC - 1))
+                nc.tensor.matmul(zs[:, s, :], lhsT=kept[(n, j // 2)][:, j % 2, batch], rhs=ident_f[:], is_transpose=True, start=False, stop=False)
+                nc.tensor.matmul(zs[:, s, :], lhsT=news[(n, j // 2)][:, j % 2, batch], rhs=ident_f[:], is_transpose=True, start=False, stop=(s == TPC - 1))
             zss[(n, j)] = zs
 
         def turn_output_gate(n, j):
             zo = psum.tile([P, TPC, P], F32, name="zo", tag="zo", bufs=2)
             for s in range(TPC):
-                nc.tensor.transpose(zo[:, s, :], acts[(n, j, GATE_O)][:, P * s:P * (s + 1)], ident_f[:])
+                nc.tensor.transpose(zo[:, s, :], acts[(n, j // 2, GATE_O)][:, j % 2, P * s:P * (s + 1)], ident_f[:])
             zos[(n, j)] = zo
-
-        tcns = {}
 
         def tanh_cell(n, j):
             t = work.tile([P, TPC, P], F32, name="tcn", tag="tcn")
             nc.scalar.activation(out=t[:], in_=zss[(n, j)][:], func=ACT.Tanh)
             tcns[(n, j)] = t
 
-        def outputs(n, j):
-            hs, cs = staged[n]
+        def store(which, n, cols):
+            rows = slice(TPC * n, TPC * (n + 1))
+            nc.sync.dma_start(out=outs[which][:, rows, cols], in_=staged[n][which][:, :, cols])
+
+        def cell_out(n, j, alone=False):
             cols = slice(P * j, P * (j + 1))
-            nc.vector.scalar_tensor_tensor(out=cs[:, :, cols], in0=zss[(n, j)][:], scalar=0.8, in1=c02s[(n, j)][:], op0=ALU.mult, op1=ALU.add)
-            hn8 = work.tile([P, TPC, P], F32, name="hn8", tag="hn8")
-            nc.vector.scalar_tensor_tensor(out=hn8[:], in0=zos[(n, j)][:], scalar=0.8, in1=tcns[(n, j)][:], op0=ALU.mult, op1=ALU.mult)
-            nc.vector.scalar_tensor_tensor(out=hs[:, :, cols], in0=sb[(HID, n)][:, :, cols], scalar=0.2, in1=hn8[:], op0=ALU.mult, op1=ALU.add)
-            if j >= 1:
-                part = slice(0, 2 * P) if j == 1 else cols
-                rows = slice(TPC * n, TPC * (n + 1))
-                nc.sync.dma_start(out=outs[1][:, rows, part], in_=cs[:, :, part])
-                nc.sync.dma_start(out=outs[0][:, rows, part], in_=hs[:, :, part])
+            inner = slice(P * (j % 2), P * (j % 2 + 1))
+            nc.vector.scalar_tensor_tensor(out=staged[n][1][:, :, cols], in0=zss[(n, j)][:], scalar=0.8, in1=c02s[(n, j // 2)][:, :, inner], op0=ALU.mult, op1=ALU.add)
+            if alone:
+                store(1, n, cols)
+            elif j % 2 == 1:
+                store(1, n, slice(P * (j - 1), P * (j + 1)))
 
-        for q in range(2):
-            turn_rows(X, 0, q)
-        for q in range(2):
-            turn_rows(HID, 0, q)
-        bias_t = psum.tile([P, P], BF16, name="bias_t", tag="ct")
-        nc.tensor.transpose(bias_t[:], bias_rows[:], ident_b[:])
-        for q in range(2):
-            quantise_rows(X, 0, q)
-        for q in range(2):
-            quantise_rows(HID, 0, q)
-        bias_col = const.tile([P, 16], F32, name="bias_col")
-        nc.vector.tensor_copy(out=bias_col[:], in_=bias_t[:, 0:16])
+        def hidden_part(n, j):
+            if j % 2 == 0:
+                hn8s[(n, j // 2)] = work.tile([P, TPC, 2 * P], F32, name="hn8", tag="hn8", bufs=2)
+            inner = slice(P * (j % 2), P * (j % 2 + 1))
+            nc.vector.scalar_tensor_tensor(out=hn8s[(n, j // 2)][:, :, inner], in0=zos[(n, j)][:], scalar=0.8, in1=tcns[(n, j)][:], op0=ALU.mult, op1=ALU.mult)
 
-        for g, gate in enumerate(GATE_ORDER):
-            regroup(0, gate, None, "v")
-            regroup(1, gate, 1, "s")
-            regroup(1, gate, 0, "v")
-            quantise_weights(0, gate)
-            quantise_weights(1, gate, 0)
-            for j in {1: (0, 1), 2: (2, 3)}.get(g, ()):
-                keep(0, j)
-            if g == 3:
-                new(0, 0)
-                new(0, 1)
-            quantise_weights(1, gate, 1)
-            for j in range(NJ):
-                for w in range(2):
-                    mx_pass(0, j, gate, w)
-            if g < 2:
-                turn_cells(0, 2 * g)
-            for j in range(NJ):
-                gate_act(0, j, gate)
-            if g == 2:
-                fifth_of_cell(0, 0)
-        for j in (2, 3):
-            new(0, j)
-        for o in (X, HID):
+        def hidden_out(n, half, i=None):
+            cols = slice(2 * P * half, 2 * P * (half + 1)) if i is None else slice(P * (2 * half + i), P * (2 * half + i + 1))
+            inner = slice(0, 2 * P) if i is None else slice(P * i, P * (i + 1))
+            nc.vector.scalar_tensor_tensor(out=staged[n][0][:, :, cols], in0=sb[(HID, n)][:, :, cols], scalar=0.2, in1=hn8s[(n, half)][:, :, inner], op0=ALU.mult, op1=ALU.add)
+            store(0, n, cols)
+
+        def mx(n, half, gate):
+            for j in (2 * half, 2 * half + 1):
+                mx_pass(n, j, gate, 0)
+                mx_pass(n, j, gate, 1)
+                gate_act(n, j, gate)
+
+        def mx1(n, j, gate):
+            mx_pass(n, j, gate, 0)
+            mx_pass(n, j, gate, 1)
+            gate_act(n, j, gate)
+
+        def turn_both(o, n):
             for q in range(2):
-                turn_rows(o, 1, q)
-        sums(0, 0)
-        turn_output_gate(0, 0)
-        for o in (X, HID):
-            for q in range(2):
-                quantise_rows(o, 1, q)
-        tanh_cell(0, 0)
+                turn_rows(o, n, q)
 
-        UNITS = ((0, 0), (0, 1), (1, 0), (0, 2), (1, 1), (0, 3), (1, 2), (1, 3))
+        def quantise_both(o, n):
+            for q in range(2):
+                quantise_rows(o, n, q)
 
         def stage_one(n, j):
             sums(n, j)
             turn_output_gate(n, j)
             tanh_cell(n, j)
 
-        fifth_of_cell(*UNITS[1])
-        for j in range(NJ):
-            if j % 2 == 0:
-                turn_cells(1, j)
-            for gate in GATE_ORDER:
-                mx_pass(1, j, gate, 0)
-                mx_pass(1, j, gate, 1)
-                gate_act(1, j, gate)
-            outputs(*UNITS[2 * j])
-            keep(1, j)
-            new(1, j)
-            for u in (2 * j + 1, 2 * j + 2):
-                if u < 8:
-                    stage_one(*UNITS[u])
-                    if u + 1 < 8:
-                        fifth_of_cell(*UNITS[u + 1])
-                    if u % 2:
-                        outputs(*UNITS[u])
+        bias_t = psum.tile([P, P], BF16, name="bias_t", tag="ct")
+        regroup(GATE_F, 0, "v")
+        quantise_weights(GATE_F, 0)
+        turn_both(X, 0)
+        turn_both(HID, 0)
+        nc.tensor.transpose(bias_t[:], bias_rows[:], ident_b[:])
+        quantise_both(X, 0)
+        bias_col = const.tile([P, 16], F32, name="bias_col")
+        nc.vector.tensor_copy(out=bias_col[:], in_=bias_t[:, 0:16])
+        regroup(GATE_I, 0, "v")
+        quantise_both(HID, 0)
+        quantise_weights(GATE_I, 0)
+        mx(0, 0, GATE_F)
+        mx(0, 0, GATE_I)
+        turn_cells(0, 0)
+        turn_both(X, 1)
+        regroup(GATE_G, 0, "v")
+        quantise_weights(GATE_G, 0)
+        keep(0, 0)
+        turn_both(HID, 1)
+        regroup(GATE_O, 0, "v")
+        quantise_both(X, 1)
+        quantise_weights(GATE_O, 0)
+        quantise_both(HID, 1)
+        mx(0, 0, GATE_G)
+        new(0, 0)
+        mx(1, 0, GATE_F)
+        turn_cells(1, 0)
+        mx(1, 0, GATE_I)
+        mx(0, 0, GATE_O)
+        mx(1, 0, GATE_G)
+        regroup(GATE_F, 1, "v")
+        keep(1, 0)
+        quantise_weights(GATE_F, 1)
+        fifth_of_cell(0, 0, "v")
+        stage_one(0, 0)
+        regroup(GATE_I, 1, "v")
+        fifth_of_cell(1, 0, "v")
+        new(1, 0)
+        quantise_weights(GATE_I, 1)
+        mx(1, 0, GATE_O)
+        cell_out(0, 0)
+        stage_one(0, 1)
+        regroup(GATE_G, 1, "s")
+        hidden_part(0, 0)
+        cell_out(0, 1)
+        hidden_part(0, 1)
+        turn_cells(0, 1)
+        regroup(GATE_O, 1, "v")
+        hidden_out(0, 0)
+        quantise_weights(GATE_G, 1)
+        mx(0, 1, GATE_F)
+        mx(0, 1, GATE_I)
+        quantise_weights(GATE_O, 1)
+        keep(0, 1)
+        stage_one(1, 0)
+        mx(0, 1, GATE_G)
+        stage_one(1, 1)
+        fifth_of_cell(0, 1, "s")
+        turn_cells(1, 1)
+        mx(0, 1, GATE_O)
+        cell_out(1, 0)
+        hidden_part(1, 0)
+        new(0, 1)
+        cell_out(1, 1)
+        hidden_part(1, 1)
+        hidden_out(1, 0)
+        mx1(1, 2, GATE_F)
+        mx1(1, 2, GATE_I)
+        stage_one(0, 2)
+        mx1(1, 2, GATE_G)
+        mx1(1, 2, GATE_O)
+        keep(1, 1, 0)
+        cell_out(0, 2)
+        hidden_part(0, 2)
+        new(1, 1, 0)
+        hidden_out(0, 1, 0)
+        mx1(1, 3, GATE_F)
+        mx1(1, 3, GATE_I)
+        stage_one(0, 3)
+        keep(1, 1, 1)
+        mx1(1, 3, GATE_G)
+        cell_out(0, 3)
+        fifth_of_cell(1, 1, "s")
+        stage_one(1, 2)
+        mx1(1, 3, GATE_O)
+        hidden_part(0, 3)
+        new(1, 1, 1)
+        hidden_out(0, 1, 1)
+        cell_out(1, 2, True)
+        hidden_part(1, 2)
+        hidden_out(1, 1, 0)
+        stage_one(1, 3)
+        cell_out(1, 3, True)
+        hidden_part(1, 3)
+        hidden_out(1, 1, 1)

@@ -111,12 +111,14 @@ def tile_lstmcell_pb_kernel(tc, x, h, c, mem_read, W_ih, W_hh, bias, out_0, out_
         w_codes = {}
         w_scales = {}
 
-        def regroup(gate, half, engine):
-            w_grouped[(gate, half)] = wgp.tile([P, 4 * P, 4], BF16, name="wg%d%d" % (gate, half), tag="wg", align_bytes=64)
-            w_codes[(gate, half)] = codes.tile([P, 4 * P], U32, name="wcode%d%d" % (gate, half), align_bytes=64)
-            w_scales[(gate, half)] = codes.tile([P, 4 * P], U8, name="wscale%d%d" % (gate, half), align_bytes=64)
-            dst = w_grouped[(gate, half)][:].rearrange("p (cc i) t -> p cc t i", i=4)
-            src = wraw[(gate, half)][:].rearrange("p t w (cm i) -> p (w cm) t i", i=4)
+        def regroup(gate, half, engine, w=None):
+            if not w:
+                w_grouped[(gate, half)] = wgp.tile([P, 4 * P, 4], BF16, name="wg%d%d" % (gate, half), tag="wg", align_bytes=64)
+                w_codes[(gate, half)] = codes.tile([P, 4 * P], U32, name="wcode%d%d" % (gate, half), align_bytes=64)
+                w_scales[(gate, half)] = codes.tile([P, 4 * P], U8, name="wscale%d%d" % (gate, half), align_bytes=64)
+            cols = slice(0, 4 * P) if w is None else slice(2 * P * w, 2 * P * (w + 1))
+            dst = w_grouped[(gate, half)][:, cols, :].rearrange("p (cc i) t -> p cc t i", i=4)
+            src = wraw[(gate, half)][:].rearrange("p t w (cm i) -> p (w cm) t i", i=4)[:, 2 * P * (w or 0) // 4:(2 * P * (w or 0) + (4 * P if w is None else 2 * P)) // 4]
             if engine == "s":
                 nc.scalar.copy(out=dst, in_=src)
             else:
@@ -173,10 +175,11 @@ def tile_lstmcell_pb_kernel(tc, x, h, c, mem_read, W_ih, W_hh, bias, out_0, out_
             nc.vector.tensor_tensor(out=kept[(n, half)][:, which, :], in0=acts[(n, half, GATE_F)][:, which, :], in1=cts[(n, half)][:, which, :], op=ALU.mult)
 
         def new(n, half, i=None):
+            engine = nc.gpsimd if half else nc.vector
             which = slice(0, 2) if i is None else slice(i, i + 1)
             if not i:
                 news[(n, half)] = work.tile([P, 2, TPC * P], F32, name="new", tag="new", bufs=2)
-            nc.vector.tensor_tensor(out=news[(n, half)][:, which, :], in0=acts[(n, half, GATE_I)][:, which, :], in1=acts[(n, half, GATE_G)][:, which, :], op=ALU.mult)
+            engine.tensor_tensor(out=news[(n, half)][:, which, :], in0=acts[(n, half, GATE_I)][:, which, :], in1=acts[(n, half, GATE_G)][:, which, :], op=ALU.mult)
 
         def fifth_of_cell(n, half, engine):
             t = work.tile([P, TPC, 2 * P], F32, name="c02", tag="c02", bufs=3)
@@ -282,6 +285,7 @@ def tile_lstmcell_pb_kernel(tc, x, h, c, mem_read, W_ih, W_hh, bias, out_0, out_
         quantise_both(HID, 1)
         mx(0, 0, GATE_G)
         new(0, 0)
+        fifth_of_cell(0, 0, "s")
         mx(1, 0, GATE_F)
         turn_cells(1, 0)
         mx(1, 0, GATE_I)
@@ -290,36 +294,35 @@ def tile_lstmcell_pb_kernel(tc, x, h, c, mem_read, W_ih, W_hh, bias, out_0, out_
         regroup(GATE_F, 1, "v")
         keep(1, 0)
         quantise_weights(GATE_F, 1)
-        fifth_of_cell(0, 0, "v")
         stage_one(0, 0)
         regroup(GATE_I, 1, "v")
-        fifth_of_cell(1, 0, "v")
         new(1, 0)
         quantise_weights(GATE_I, 1)
         mx(1, 0, GATE_O)
-        cell_out(0, 0)
         stage_one(0, 1)
-        regroup(GATE_G, 1, "s")
-        hidden_part(0, 0)
-        cell_out(0, 1)
-        hidden_part(0, 1)
-        turn_cells(0, 1)
-        regroup(GATE_O, 1, "v")
-        hidden_out(0, 0)
+        regroup(GATE_G, 1, "v")
         quantise_weights(GATE_G, 1)
+        cell_out(0, 0)
+        hidden_part(0, 0)
+        turn_cells(0, 1)
+        fifth_of_cell(1, 0, "s")
         mx(0, 1, GATE_F)
+        regroup(GATE_O, 1, "v")
         mx(0, 1, GATE_I)
+        cell_out(0, 1)
         quantise_weights(GATE_O, 1)
+        hidden_part(0, 1)
         keep(0, 1)
-        stage_one(1, 0)
         mx(0, 1, GATE_G)
+        stage_one(1, 0)
+        mx(0, 1, GATE_O)
         stage_one(1, 1)
+        hidden_out(0, 0)
+        new(0, 1)
         fifth_of_cell(0, 1, "s")
         turn_cells(1, 1)
-        mx(0, 1, GATE_O)
         cell_out(1, 0)
         hidden_part(1, 0)
-        new(0, 1)
         cell_out(1, 1)
         hidden_part(1, 1)
         hidden_out(1, 0)

@@ -32,7 +32,7 @@ def tile_lstmcell_pb_kernel(tc, x, h, c, mem_read, W_ih, W_hh, bias, out_0, out_
         inp = ctx.enter_context(tc.tile_pool(name="inp", bufs=1))
         wrawp = ctx.enter_context(tc.tile_pool(name="wraw", bufs=1))
         wgp = ctx.enter_context(tc.tile_pool(name="wg", bufs=4))
-        agp = ctx.enter_context(tc.tile_pool(name="ag", bufs=4))
+        agp = ctx.enter_context(tc.tile_pool(name="ag", bufs=2))
         codes = ctx.enter_context(tc.tile_pool(name="codes", bufs=1))
         work = ctx.enter_context(tc.tile_pool(name="work", bufs=3))
         stage = ctx.enter_context(tc.tile_pool(name="stage", bufs=1))
@@ -49,14 +49,13 @@ def tile_lstmcell_pb_kernel(tc, x, h, c, mem_read, W_ih, W_hh, bias, out_0, out_
             nc.sync.dma_start(out=t[:], in_=views[which][:, TPC * n:TPC * (n + 1), :])
             sb[(which, n)] = t
 
-        def load_weights(gate, half):
-            t = wrawp.tile([P, 4, 2, 2 * P], BF16, name="wraw%d%d" % (gate, half))
+        def load_weights(gate, half, w):
+            if w == 0:
+                wraw[(gate, half)] = wrawp.tile([P, 4, 2, 2 * P], BF16, name="wraw%d%d" % (gate, half))
             first = H * gate + 2 * P * half
-            for w in range(2):
-                for u in range(2):
-                    src = (W_ih, W_hh)[w][256 * u:256 * (u + 1), first:first + 2 * P].rearrange("(p e) n -> p e n", e=2)
-                    nc.sync.dma_start(out=t[:, 2 * u:2 * u + 2, w, :], in_=src)
-            wraw[(gate, half)] = t
+            for u in range(2):
+                src = (W_ih, W_hh)[w][256 * u:256 * (u + 1), first:first + 2 * P].rearrange("(p e) n -> p e n", e=2)
+                nc.sync.dma_start(out=wraw[(gate, half)][:, 2 * u:2 * u + 2, w, :], in_=src)
 
         warm = const.tile([P, 1], F32, name="warm")
         nc.vector.memset(warm[:], 0.0)
@@ -65,21 +64,25 @@ def tile_lstmcell_pb_kernel(tc, x, h, c, mem_read, W_ih, W_hh, bias, out_0, out_
 
         bias_rows = const.tile([P, P], BF16, name="bias_rows")
         nc.vector.memset(bias_rows[:], 0.0)
-        load_weights(GATE_F, 0)
         load_rows(X, 0)
-        nc.sync.dma_start(out=bias_rows[0:16, :], in_=bias.rearrange("(t m) -> t m", m=P))
+        load_weights(GATE_F, 0, 0)
         load_rows(HID, 0)
-        load_weights(GATE_I, 0)
-        load_weights(GATE_G, 0)
+        load_weights(GATE_F, 0, 1)
+        nc.sync.dma_start(out=bias_rows[0:16, :], in_=bias.rearrange("(t m) -> t m", m=P))
+        for gate in (GATE_I, GATE_G):
+            for w in range(2):
+                load_weights(gate, 0, w)
         load_rows(CELL, 0)
         load_rows(X, 1)
         load_rows(HID, 1)
-        load_weights(GATE_O, 0)
+        for w in range(2):
+            load_weights(GATE_O, 0, w)
         load_rows(CELL, 1)
         load_rows(MEM, 0)
-        load_rows(MEM, 1)
         for gate in GATE_ORDER:
-            load_weights(gate, 1)
+            for w in range(2):
+                load_weights(gate, 1, w)
+        load_rows(MEM, 1)
 
         ident_f = const.tile([P, P], F32, name="ident_f")
         make_identity(nc, ident_f[:])
@@ -124,8 +127,9 @@ def tile_lstmcell_pb_kernel(tc, x, h, c, mem_read, W_ih, W_hh, bias, out_0, out_
             else:
                 nc.vector.tensor_copy(out=dst, in_=src)
 
-        def quantise_weights(gate, half):
-            nc.vector.quantize_mx(out=w_codes[(gate, half)][:].bitcast(FP8X4), scales=w_scales[(gate, half)][:], in_=w_grouped[(gate, half)][:].rearrange("p cm t -> p (cm t)"))
+        def quantise_weights(gate, half, w=None):
+            cols = slice(0, 4 * P) if w is None else slice(2 * P * w, 2 * P * (w + 1))
+            nc.vector.quantize_mx(out=w_codes[(gate, half)][:, cols].bitcast(FP8X4), scales=w_scales[(gate, half)][:, cols], in_=w_grouped[(gate, half)][:, cols, :].rearrange("p cm t -> p (cm t)"))
 
         staged = {}
         for n in range(NCHUNK):
@@ -181,6 +185,15 @@ def tile_lstmcell_pb_kernel(tc, x, h, c, mem_read, W_ih, W_hh, bias, out_0, out_
                 news[(n, half)] = work.tile([P, 2, TPC * P], F32, name="new", tag="new", bufs=2)
             engine.tensor_tensor(out=news[(n, half)][:, which, :], in0=acts[(n, half, GATE_I)][:, which, :], in1=acts[(n, half, GATE_G)][:, which, :], op=ALU.mult)
 
+        totals = {}
+
+        def total(n, half, i=None):
+            which = slice(0, 2) if i is None else slice(i, i + 1)
+            t = work.tile([P, 2, TPC * P], F32, name="total", tag="total", bufs=1)
+            nc.gpsimd.tensor_tensor(out=t[:, which, :], in0=kept[(n, half)][:, which, :], in1=news[(n, half)][:, which, :], op=ALU.add)
+            for part in range(2)[which]:
+                totals[(n, 2 * half + part)] = t
+
         def fifth_of_cell(n, half, engine):
             t = work.tile([P, TPC, 2 * P], F32, name="c02", tag="c02", bufs=3)
             src = sb[(CELL, n)][:, :, 2 * P * half:2 * P * (half + 1)]
@@ -193,10 +206,10 @@ def tile_lstmcell_pb_kernel(tc, x, h, c, mem_read, W_ih, W_hh, bias, out_0, out_
         def sums(n, j):
             zs = psum.tile([P, TPC, P], F32, name="zs", tag="zs", bufs=2)
             nc.tensor.matmul(zs[:], lhsT=ident_b[:], rhs=sb[(MEM, n)][:, :, P * j:P * (j + 1)], start=True, stop=False)
+            parts = [totals[(n, j)]] if (n, j) in totals else [kept[(n, j // 2)], news[(n, j // 2)]]
             for s in range(TPC):
-                batch = slice(P * s, P * (s + 1))
-                nc.tensor.matmul(zs[:, s, :], lhsT=kept[(n, j // 2)][:, j % 2, batch], rhs=ident_f[:], is_transpose=True, start=False, stop=False)
-                nc.tensor.matmul(zs[:, s, :], lhsT=news[(n, j // 2)][:, j % 2, batch], rhs=ident_f[:], is_transpose=True, start=False, stop=(s == TPC - 1))
+                for part in parts:
+                    nc.tensor.matmul(zs[:, s, :], lhsT=part[:, j % 2, P * s:P * (s + 1)], rhs=ident_f[:], is_transpose=True, start=False, stop=(s == TPC - 1 and part is parts[-1]))
             zss[(n, j)] = zs
 
         def turn_output_gate(n, j):
@@ -260,18 +273,24 @@ def tile_lstmcell_pb_kernel(tc, x, h, c, mem_read, W_ih, W_hh, bias, out_0, out_
             tanh_cell(n, j)
 
         bias_t = psum.tile([P, P], BF16, name="bias_t", tag="ct")
-        regroup(GATE_F, 0, "v")
-        quantise_weights(GATE_F, 0)
         turn_both(X, 0)
+        regroup(GATE_F, 0, "v", 0)
+        quantise_both(X, 0)
+        quantise_weights(GATE_F, 0, 0)
         turn_both(HID, 0)
         nc.tensor.transpose(bias_t[:], bias_rows[:], ident_b[:])
-        quantise_both(X, 0)
+        regroup(GATE_F, 0, "v", 1)
+        quantise_both(HID, 0)
+        quantise_weights(GATE_F, 0, 1)
         bias_col = const.tile([P, 16], F32, name="bias_col")
         nc.vector.tensor_copy(out=bias_col[:], in_=bias_t[:, 0:16])
         regroup(GATE_I, 0, "v")
-        quantise_both(HID, 0)
         quantise_weights(GATE_I, 0)
-        mx(0, 0, GATE_F)
+        for w in range(2):
+            for j in range(2):
+                mx_pass(0, j, GATE_F, w)
+        for j in range(2):
+            gate_act(0, j, GATE_F)
         mx(0, 0, GATE_I)
         turn_cells(0, 0)
         turn_both(X, 1)
@@ -279,11 +298,11 @@ def tile_lstmcell_pb_kernel(tc, x, h, c, mem_read, W_ih, W_hh, bias, out_0, out_
         quantise_weights(GATE_G, 0)
         keep(0, 0)
         turn_both(HID, 1)
-        regroup(GATE_O, 0, "v")
         quantise_both(X, 1)
-        quantise_weights(GATE_O, 0)
         quantise_both(HID, 1)
+        regroup(GATE_O, 0, "v")
         mx(0, 0, GATE_G)
+        quantise_weights(GATE_O, 0)
         new(0, 0)
         fifth_of_cell(0, 0, "s")
         mx(1, 0, GATE_F)
@@ -319,6 +338,7 @@ def tile_lstmcell_pb_kernel(tc, x, h, c, mem_read, W_ih, W_hh, bias, out_0, out_
         stage_one(1, 1)
         hidden_out(0, 0)
         new(0, 1)
+        total(0, 1)
         fifth_of_cell(0, 1, "s")
         turn_cells(1, 1)
         cell_out(1, 0)

@@ -19,6 +19,7 @@ NCHUNK = 2
 TPC = 4
 NJ = 4
 GATE_F, GATE_I, GATE_O, GATE_G = 0, 1, 2, 3
+ALL = slice(0, TPC)
 FUNC = {GATE_F: ACT.Sigmoid, GATE_I: ACT.Sigmoid, GATE_G: ACT.Tanh, GATE_O: ACT.Sigmoid}
 TAG = {GATE_F: "gf", GATE_I: "gi", GATE_G: "gg", GATE_O: "go"}
 GATE_ORDER = (GATE_F, GATE_I, GATE_G, GATE_O)
@@ -65,10 +66,10 @@ def tile_lstmcell_pb_kernel(tc, x, h, c, mem_read, W_ih, W_hh, bias, out_0, out_
         bias_rows = const.tile([P, P], BF16, name="bias_rows")
         nc.vector.memset(bias_rows[:], 0.0)
         load_rows(X, 0)
+        nc.sync.dma_start(out=bias_rows[0:16, :], in_=bias.rearrange("(t m) -> t m", m=P))
         load_weights(GATE_F, 0, 0)
         load_rows(HID, 0)
         load_weights(GATE_F, 0, 1)
-        nc.sync.dma_start(out=bias_rows[0:16, :], in_=bias.rearrange("(t m) -> t m", m=P))
         for gate in (GATE_I, GATE_G):
             for w in range(2):
                 load_weights(gate, 0, w)
@@ -200,53 +201,53 @@ def tile_lstmcell_pb_kernel(tc, x, h, c, mem_read, W_ih, W_hh, bias, out_0, out_
             if engine == "s":
                 nc.scalar.activation(out=t[:], in_=src, func=ACT.Copy, scale=0.2)
             else:
-                nc.vector.tensor_scalar(out=t[:], in0=src, scalar1=0.2, scalar2=0.0, op0=ALU.mult, op1=ALU.add)
+                nc.gpsimd.tensor_scalar(out=t[:], in0=src, scalar1=0.2, scalar2=0.0, op0=ALU.mult, op1=ALU.add)
             c02s[(n, half)] = t
 
-        def sums(n, j):
+        def sums(n, j, rows):
             zs = psum.tile([P, TPC, P], F32, name="zs", tag="zs", bufs=2)
-            nc.tensor.matmul(zs[:], lhsT=ident_b[:], rhs=sb[(MEM, n)][:, :, P * j:P * (j + 1)], start=True, stop=False)
+            nc.tensor.matmul(zs[:, rows, :], lhsT=ident_b[:], rhs=sb[(MEM, n)][:, rows, P * j:P * (j + 1)], start=True, stop=False)
             parts = [totals[(n, j)]] if (n, j) in totals else [kept[(n, j // 2)], news[(n, j // 2)]]
-            for s in range(TPC):
+            for s in range(TPC)[rows]:
                 for part in parts:
-                    nc.tensor.matmul(zs[:, s, :], lhsT=part[:, j % 2, P * s:P * (s + 1)], rhs=ident_f[:], is_transpose=True, start=False, stop=(s == TPC - 1 and part is parts[-1]))
-            zss[(n, j)] = zs
+                    last = s == rows.stop - 1 and part is parts[-1]
+                    nc.tensor.matmul(zs[:, s, :], lhsT=part[:, j % 2, P * s:P * (s + 1)], rhs=ident_f[:], is_transpose=True, start=False, stop=last)
+            zss[(n, j, rows.start)] = zs
 
-        def turn_output_gate(n, j):
+        def turn_output_gate(n, j, rows):
             zo = psum.tile([P, TPC, P], F32, name="zo", tag="zo", bufs=2)
-            for s in range(TPC):
+            for s in range(TPC)[rows]:
                 nc.tensor.transpose(zo[:, s, :], acts[(n, j // 2, GATE_O)][:, j % 2, P * s:P * (s + 1)], ident_f[:])
-            zos[(n, j)] = zo
+            zos[(n, j, rows.start)] = zo
 
-        def tanh_cell(n, j):
+        def tanh_cell(n, j, rows):
             t = work.tile([P, TPC, P], F32, name="tcn", tag="tcn")
-            nc.scalar.activation(out=t[:], in_=zss[(n, j)][:], func=ACT.Tanh)
-            tcns[(n, j)] = t
+            nc.scalar.activation(out=t[:, rows, :], in_=zss[(n, j, rows.start)][:, rows, :], func=ACT.Tanh)
+            tcns[(n, j, rows.start)] = t
 
-        def store(which, n, cols):
-            rows = slice(TPC * n, TPC * (n + 1))
-            nc.sync.dma_start(out=outs[which][:, rows, cols], in_=staged[n][which][:, :, cols])
+        def store(which, n, cols, rows=ALL):
+            nc.sync.dma_start(out=outs[which][:, TPC * n + rows.start:TPC * n + rows.stop, cols], in_=staged[n][which][:, rows, cols])
 
-        def cell_out(n, j, alone=False):
+        def cell_out(n, j, alone=False, rows=ALL):
             cols = slice(P * j, P * (j + 1))
             inner = slice(P * (j % 2), P * (j % 2 + 1))
-            nc.vector.scalar_tensor_tensor(out=staged[n][1][:, :, cols], in0=zss[(n, j)][:], scalar=0.8, in1=c02s[(n, j // 2)][:, :, inner], op0=ALU.mult, op1=ALU.add)
+            nc.vector.scalar_tensor_tensor(out=staged[n][1][:, rows, cols], in0=zss[(n, j, rows.start)][:, rows, :], scalar=0.8, in1=c02s[(n, j // 2)][:, rows, inner], op0=ALU.mult, op1=ALU.add)
             if alone:
-                store(1, n, cols)
+                store(1, n, cols, rows)
             elif j % 2 == 1:
                 store(1, n, slice(P * (j - 1), P * (j + 1)))
 
-        def hidden_part(n, j):
-            if j % 2 == 0:
+        def hidden_part(n, j, rows=ALL):
+            if (n, j // 2) not in hn8s:
                 hn8s[(n, j // 2)] = work.tile([P, TPC, 2 * P], F32, name="hn8", tag="hn8", bufs=2)
             inner = slice(P * (j % 2), P * (j % 2 + 1))
-            nc.vector.scalar_tensor_tensor(out=hn8s[(n, j // 2)][:, :, inner], in0=zos[(n, j)][:], scalar=0.8, in1=tcns[(n, j)][:], op0=ALU.mult, op1=ALU.mult)
+            nc.vector.scalar_tensor_tensor(out=hn8s[(n, j // 2)][:, rows, inner], in0=zos[(n, j, rows.start)][:, rows, :], scalar=0.8, in1=tcns[(n, j, rows.start)][:, rows, :], op0=ALU.mult, op1=ALU.mult)
 
-        def hidden_out(n, half, i=None):
+        def hidden_out(n, half, i=None, rows=ALL):
             cols = slice(2 * P * half, 2 * P * (half + 1)) if i is None else slice(P * (2 * half + i), P * (2 * half + i + 1))
             inner = slice(0, 2 * P) if i is None else slice(P * i, P * (i + 1))
-            nc.vector.scalar_tensor_tensor(out=staged[n][0][:, :, cols], in0=sb[(HID, n)][:, :, cols], scalar=0.2, in1=hn8s[(n, half)][:, :, inner], op0=ALU.mult, op1=ALU.add)
-            store(0, n, cols)
+            nc.vector.scalar_tensor_tensor(out=staged[n][0][:, rows, cols], in0=sb[(HID, n)][:, rows, cols], scalar=0.2, in1=hn8s[(n, half)][:, rows, inner], op0=ALU.mult, op1=ALU.add)
+            store(0, n, cols, rows)
 
         def mx(n, half, gate):
             for j in (2 * half, 2 * half + 1):
@@ -267,24 +268,25 @@ def tile_lstmcell_pb_kernel(tc, x, h, c, mem_read, W_ih, W_hh, bias, out_0, out_
             for q in range(2):
                 quantise_rows(o, n, q)
 
-        def stage_one(n, j):
-            sums(n, j)
-            turn_output_gate(n, j)
-            tanh_cell(n, j)
+        def stage_one(n, j, rows=ALL):
+            sums(n, j, rows)
+            turn_output_gate(n, j, rows)
+            tanh_cell(n, j, rows)
 
         bias_t = psum.tile([P, P], BF16, name="bias_t", tag="ct")
         turn_both(X, 0)
+        nc.tensor.transpose(bias_t[:], bias_rows[:], ident_b[:])
         regroup(GATE_F, 0, "v", 0)
         quantise_both(X, 0)
         quantise_weights(GATE_F, 0, 0)
+        bias_col = const.tile([P, 16], F32, name="bias_col")
+        nc.vector.tensor_copy(out=bias_col[:], in_=bias_t[:, 0:16])
         turn_both(HID, 0)
-        nc.tensor.transpose(bias_t[:], bias_rows[:], ident_b[:])
         regroup(GATE_F, 0, "v", 1)
         quantise_both(HID, 0)
         quantise_weights(GATE_F, 0, 1)
-        bias_col = const.tile([P, 16], F32, name="bias_col")
-        nc.vector.tensor_copy(out=bias_col[:], in_=bias_t[:, 0:16])
-        regroup(GATE_I, 0, "v")
+        regroup(GATE_I, 0, "s", 0)
+        regroup(GATE_I, 0, "v", 1)
         quantise_weights(GATE_I, 0)
         for w in range(2):
             for j in range(2):
@@ -355,6 +357,7 @@ def tile_lstmcell_pb_kernel(tc, x, h, c, mem_read, W_ih, W_hh, bias, out_0, out_
         cell_out(0, 2)
         hidden_part(0, 2)
         new(1, 1, 0)
+        fifth_of_cell(1, 1, "g")
         hidden_out(0, 1, 0)
         mx1(1, 3, GATE_F)
         mx1(1, 3, GATE_I)
@@ -362,7 +365,6 @@ def tile_lstmcell_pb_kernel(tc, x, h, c, mem_read, W_ih, W_hh, bias, out_0, out_
         keep(1, 1, 1)
         mx1(1, 3, GATE_G)
         cell_out(0, 3)
-        fifth_of_cell(1, 1, "s")
         stage_one(1, 2)
         mx1(1, 3, GATE_O)
         hidden_part(0, 3)
@@ -371,7 +373,11 @@ def tile_lstmcell_pb_kernel(tc, x, h, c, mem_read, W_ih, W_hh, bias, out_0, out_
         cell_out(1, 2, True)
         hidden_part(1, 2)
         hidden_out(1, 1, 0)
-        stage_one(1, 3)
-        cell_out(1, 3, True)
-        hidden_part(1, 3)
-        hidden_out(1, 1, 1)
+        halves = (slice(0, 2), slice(2, 4))
+        for rows in halves:
+            stage_one(1, 3, rows)
+        for rows in halves:
+            cell_out(1, 3, True, rows)
+            hidden_part(1, 3, rows)
+        for rows in halves:
+            hidden_out(1, 1, 1, rows)

@@ -20,6 +20,7 @@ TPC = 4
 NJ = 4
 GATE_F, GATE_I, GATE_O, GATE_G = 0, 1, 2, 3
 ALL = slice(0, TPC)
+RUN = 8
 FUNC = {GATE_F: ACT.Sigmoid, GATE_I: ACT.Sigmoid, GATE_G: ACT.Tanh, GATE_O: ACT.Sigmoid}
 TAG = {GATE_F: "gf", GATE_I: "gi", GATE_G: "gg", GATE_O: "go"}
 GATE_ORDER = (GATE_F, GATE_I, GATE_G, GATE_O)
@@ -94,18 +95,21 @@ def tile_lstmcell_pb_kernel(tc, x, h, c, mem_read, W_ih, W_hh, bias, out_0, out_
         a_codes = {}
         a_scales = {}
 
-        def turn_rows(o, n, q):
+        def turn_rows(o, n, q, engine="s", bank=("acc", 3)):
             if q == 0:
                 a_grouped[(o, n)] = agp.tile([P, 4 * TPC * P], BF16, name="ag%d%d" % (o, n), tag="ag", align_bytes=64)
                 a_codes[(o, n)] = codes.tile([P, TPC * P], U32, name="acode%d%d" % (o, n), align_bytes=64)
                 a_scales[(o, n)] = codes.tile([P, TPC * P], U8, name="ascale%d%d" % (o, n), align_bytes=64)
             words = sb[(o, n)][:].bitcast(F32)
-            pt = psum.tile([P, 4, P], F32, name="acc", tag="acc", bufs=3)
+            pt = psum.tile([P, 4, P], F32, name="turned", tag=bank[0], bufs=bank[1])
             for rr in range(2):
                 for u in range(2):
                     nc.tensor.transpose(pt[:, 2 * rr + u, :], words[:, 2 * q + rr, P * u:P * (u + 1)], ident_f[:])
             dst = a_grouped[(o, n)][:].bitcast(F32)[:, 512 * q:512 * (q + 1)].rearrange("p (rr b u) -> p rr b u", rr=2, u=2)
-            nc.scalar.copy(out=dst, in_=pt[:].rearrange("p (rr u) b -> p rr b u", u=2))
+            if engine == "s":
+                nc.scalar.copy(out=dst, in_=pt[:].rearrange("p (rr u) b -> p rr b u", u=2))
+            else:
+                nc.vector.tensor_copy(out=dst, in_=pt[:].rearrange("p (rr u) b -> p rr b u", u=2))
 
         def quantise_rows(o, n, q):
             half = slice(2 * P * q, 2 * P * (q + 1))
@@ -121,8 +125,8 @@ def tile_lstmcell_pb_kernel(tc, x, h, c, mem_read, W_ih, W_hh, bias, out_0, out_
                 w_codes[(gate, half)] = codes.tile([P, 4 * P], U32, name="wcode%d%d" % (gate, half), align_bytes=64)
                 w_scales[(gate, half)] = codes.tile([P, 4 * P], U8, name="wscale%d%d" % (gate, half), align_bytes=64)
             cols = slice(0, 4 * P) if w is None else slice(2 * P * w, 2 * P * (w + 1))
-            dst = w_grouped[(gate, half)][:, cols, :].rearrange("p (cc i) t -> p cc t i", i=4)
-            src = wraw[(gate, half)][:].rearrange("p t w (cm i) -> p (w cm) t i", i=4)[:, 2 * P * (w or 0) // 4:(2 * P * (w or 0) + (4 * P if w is None else 2 * P)) // 4]
+            dst = w_grouped[(gate, half)][:, cols, :].rearrange("p (cc i) t -> p cc t i", i=RUN)
+            src = wraw[(gate, half)][:].rearrange("p t w (cm i) -> p (w cm) t i", i=RUN)[:, cols.start // RUN:cols.stop // RUN]
             if engine == "s":
                 nc.scalar.copy(out=dst, in_=src)
             else:
@@ -295,17 +299,19 @@ def tile_lstmcell_pb_kernel(tc, x, h, c, mem_read, W_ih, W_hh, bias, out_0, out_
             gate_act(0, j, GATE_F)
         mx(0, 0, GATE_I)
         turn_cells(0, 0)
-        turn_both(X, 1)
+        for q in range(2):
+            turn_rows(X, 1, q, "s", ("zs", 2))
         regroup(GATE_G, 0, "v")
         quantise_weights(GATE_G, 0)
         keep(0, 0)
-        turn_both(HID, 1)
+        for q in range(2):
+            turn_rows(HID, 1, q, "s", ("zo", 2))
         quantise_both(X, 1)
         quantise_both(HID, 1)
         regroup(GATE_O, 0, "v")
         mx(0, 0, GATE_G)
-        quantise_weights(GATE_O, 0)
         new(0, 0)
+        quantise_weights(GATE_O, 0)
         fifth_of_cell(0, 0, "s")
         mx(1, 0, GATE_F)
         turn_cells(1, 0)
@@ -350,8 +356,8 @@ def tile_lstmcell_pb_kernel(tc, x, h, c, mem_read, W_ih, W_hh, bias, out_0, out_
         hidden_out(1, 0)
         mx1(1, 2, GATE_F)
         mx1(1, 2, GATE_I)
-        stage_one(0, 2)
         mx1(1, 2, GATE_G)
+        stage_one(0, 2)
         mx1(1, 2, GATE_O)
         keep(1, 1, 0)
         cell_out(0, 2)

@@ -46,9 +46,11 @@ def tile_lstmcell_pb_kernel(tc, x, h, c, mem_read, W_ih, W_hh, bias, out_0, out_
         sb = {}
         wraw = {}
 
-        def load_rows(which, n):
+        def load_rows(which, n, parts=1):
             t = inp.tile([P, TPC, K], BF16, name="in%d%d" % (which, n))
-            nc.sync.dma_start(out=t[:], in_=views[which][:, TPC * n:TPC * (n + 1), :])
+            step = TPC // parts
+            for first in range(0, TPC, step):
+                nc.sync.dma_start(out=t[:, first:first + step, :], in_=views[which][:, TPC * n + first:TPC * n + first + step, :])
             sb[(which, n)] = t
 
         def load_weights(gate, half, w):
@@ -86,6 +88,9 @@ def tile_lstmcell_pb_kernel(tc, x, h, c, mem_read, W_ih, W_hh, bias, out_0, out_
                 load_weights(gate, 1, w)
         load_rows(MEM, 1)
 
+        zeros = const.tile([P, TPC * P], BF16, name="zeros")
+        nc.vector.memset(zeros[:], 0.0)
+
         ident_f = const.tile([P, P], F32, name="ident_f")
         make_identity(nc, ident_f[:])
         ident_b = const.tile([P, P], BF16, name="ident_b")
@@ -114,6 +119,12 @@ def tile_lstmcell_pb_kernel(tc, x, h, c, mem_read, W_ih, W_hh, bias, out_0, out_
         def quantise_rows(o, n, q):
             half = slice(2 * P * q, 2 * P * (q + 1))
             nc.vector.quantize_mx(out=a_codes[(o, n)][:, half].bitcast(FP8X4), scales=a_scales[(o, n)][:, half], in_=a_grouped[(o, n)][:, 8 * P * q:8 * P * (q + 1)])
+
+        idle = psum.tile([P, TPC * P], F32, name="idle", tag="zs", bufs=2)
+
+        def warm_up(times):
+            for repeat in range(times):
+                nc.tensor.matmul(idle[:], lhsT=zeros[:, 0:P], rhs=zeros[:], start=True, stop=True)
 
         w_grouped = {}
         w_codes = {}
@@ -278,14 +289,17 @@ def tile_lstmcell_pb_kernel(tc, x, h, c, mem_read, W_ih, W_hh, bias, out_0, out_
             tanh_cell(n, j, rows)
 
         bias_t = psum.tile([P, P], BF16, name="bias_t", tag="ct")
+        warm_up(4)
         turn_both(X, 0)
         nc.tensor.transpose(bias_t[:], bias_rows[:], ident_b[:])
+        warm_up(2)
         regroup(GATE_F, 0, "v", 0)
         quantise_both(X, 0)
         quantise_weights(GATE_F, 0, 0)
         bias_col = const.tile([P, 16], F32, name="bias_col")
         nc.vector.tensor_copy(out=bias_col[:], in_=bias_t[:, 0:16])
         turn_both(HID, 0)
+        warm_up(2)
         regroup(GATE_F, 0, "v", 1)
         quantise_both(HID, 0)
         quantise_weights(GATE_F, 0, 1)
@@ -301,6 +315,7 @@ def tile_lstmcell_pb_kernel(tc, x, h, c, mem_read, W_ih, W_hh, bias, out_0, out_
         turn_cells(0, 0)
         for q in range(2):
             turn_rows(X, 1, q, "s", ("zs", 2))
+            warm_up(1)
         regroup(GATE_G, 0, "v")
         quantise_weights(GATE_G, 0)
         keep(0, 0)

@@ -120,7 +120,7 @@ def tile_lstmcell_pb_kernel(tc, x, h, c, mem_read, W_ih, W_hh, bias, out_0, out_
             half = slice(2 * P * q, 2 * P * (q + 1))
             nc.vector.quantize_mx(out=a_codes[(o, n)][:, half].bitcast(FP8X4), scales=a_scales[(o, n)][:, half], in_=a_grouped[(o, n)][:, 8 * P * q:8 * P * (q + 1)])
 
-        idle = psum.tile([P, TPC * P], F32, name="idle", tag="zs", bufs=2)
+        idle = psum.tile([P, TPC * P], F32, name="idle", tag="zo", bufs=2)
 
         def warm_up(times):
             for repeat in range(times):
@@ -315,7 +315,6 @@ def tile_lstmcell_pb_kernel(tc, x, h, c, mem_read, W_ih, W_hh, bias, out_0, out_
         turn_cells(0, 0)
         for q in range(2):
             turn_rows(X, 1, q, "s", ("zs", 2))
-            warm_up(1)
         regroup(GATE_G, 0, "v")
         quantise_weights(GATE_G, 0)
         keep(0, 0)

from contextlib import ExitStack

import concourse.mybir as mybir
from concourse.masks import make_identity

F32 = mybir.dt.float32
BF16 = mybir.dt.bfloat16
U32 = mybir.dt.uint32
U8 = mybir.dt.uint8
FP8X4 = mybir.dt.float8_e4m3fn_x4
ACT = mybir.ActivationFunctionType
ALU = mybir.AluOpType

P = 128
B, K, H = 1024, 512, 512
FLOPS = 2 * B * (2 * K) * (4 * H)

NCHUNK = 2
TPC = 4
NJ = 4
GATE_F, GATE_I, GATE_O, GATE_G = 0, 1, 2, 3
ALL = slice(0, TPC)
RUN = 8
FUNC = {GATE_F: ACT.Sigmoid, GATE_I: ACT.Sigmoid, GATE_G: ACT.Tanh, GATE_O: ACT.Sigmoid}
TAG = {GATE_F: "gf", GATE_I: "gi", GATE_G: "gg", GATE_O: "go"}
GATE_ORDER = (GATE_F, GATE_I, GATE_G, GATE_O)
X, HID, CELL, MEM = 0, 1, 2, 3


def tile_lstmcell_pb_kernel(tc, x, h, c, mem_read, W_ih, W_hh, bias, out_0, out_1):
    nc = tc.nc
    with ExitStack() as ctx:
        const = ctx.enter_context(tc.tile_pool(name="const", bufs=1))
        inp = ctx.enter_context(tc.tile_pool(name="inp", bufs=1))
        wrawp = ctx.enter_context(tc.tile_pool(name="wraw", bufs=1))
        wgp = ctx.enter_context(tc.tile_pool(name="wg", bufs=4))
        agp = ctx.enter_context(tc.tile_pool(name="ag", bufs=2))
        codes = ctx.enter_context(tc.tile_pool(name="codes", bufs=1))
        work = ctx.enter_context(tc.tile_pool(name="work", bufs=3))
        stage = ctx.enter_context(tc.tile_pool(name="stage", bufs=1))
        psum = ctx.enter_context(tc.psum_pool(name="psum", bufs=1))
        ctx.enter_context(tc.manual_schedule())

        views = [t.rearrange("(p r) k -> p r k", r=NCHUNK * TPC) for t in (x, h, c, mem_read)]
        outs = [t.rearrange("(p r) k -> p r k", r=NCHUNK * TPC) for t in (out_0, out_1)]
        sb = {}
        wraw = {}

        def load_rows(which, n, parts=1):
            t = inp.tile([P, TPC, K], BF16, name="in%d%d" % (which, n))
            step = TPC // parts
            for first in range(0, TPC, step):
                nc.sync.dma_start(out=t[:, first:first + step, :], in_=views[which][:, TPC * n + first:TPC * n + first + step, :])
            sb[(which, n)] = t

        def load_weights(gate, half, w):
            if w == 0:
                wraw[(gate, half)] = wrawp.tile([P, 4, 2, 2 * P], BF16, name="wraw%d%d" % (gate, half))
            first = H * gate + 2 * P * half
            for u in range(2):
                src = (W_ih, W_hh)[w][256 * u:256 * (u + 1), first:first + 2 * P].rearrange("(p e) n -> p e n", e=2)
                nc.sync.dma_start(out=wraw[(gate, half)][:, 2 * u:2 * u + 2, w, :], in_=src)

        warm = const.tile([P, 1], F32, name="warm")
        nc.vector.memset(warm[:], 0.0)
        warm_out = const.tile([P, 1], F32, name="warm_out")
        nc.scalar.activation(out=warm_out[:], in_=warm[:], func=ACT.Sigmoid)

        bias_rows = const.tile([P, P], BF16, name="bias_rows")
        nc.vector.memset(bias_rows[:], 0.0)
        load_rows(X, 0)
        nc.sync.dma_start(out=bias_rows[0:16, :], in_=bias.rearrange("(t m) -> t m", m=P))
        load_weights(GATE_F, 0, 0)
        load_rows(HID, 0)
        load_weights(GATE_F, 0, 1)
        for gate in (GATE_I, GATE_G):
            for w in range(2):
                load_weights(gate, 0, w)
        load_rows(CELL, 0)
        load_rows(X, 1)
        load_rows(HID, 1)
        for w in range(2):
            load_weights(GATE_O, 0, w)
        load_rows(CELL, 1)
        load_rows(MEM, 0)
        for gate in GATE_ORDER:
            for w in range(2):
                load_weights(gate, 1, w)
        load_rows(MEM, 1)

        zeros = const.tile([P, TPC * P], BF16, name="zeros")
        nc.vector.memset(zeros[:], 0.0)

        ident_f = const.tile([P, P], F32, name="ident_f")
        make_identity(nc, ident_f[:])
        ident_b = const.tile([P, P], BF16, name="ident_b")
        make_identity(nc, ident_b[:])

        a_grouped = {}
        a_codes = {}
        a_scales = {}

        def turn_rows(o, n, q, engine="s", bank=("acc", 3)):
            if q == 0:
                a_grouped[(o, n)] = agp.tile([P, 4 * TPC * P], BF16, name="ag%d%d" % (o, n), tag="ag", align_bytes=64)
                a_codes[(o, n)] = codes.tile([P, TPC * P], U32, name="acode%d%d" % (o, n), align_bytes=64)
                a_scales[(o, n)] = codes.tile([P, TPC * P], U8, name="ascale%d%d" % (o, n), align_bytes=64)
            words = sb[(o, n)][:].bitcast(F32)
            pt = psum.tile([P, 4, P], F32, name="turned", tag=bank[0], bufs=bank[1])
            for rr in range(2):
                for u in range(2):
                    nc.tensor.transpose(pt[:, 2 * rr + u, :], words[:, 2 * q + rr, P * u:P * (u + 1)], ident_f[:])
            dst = a_grouped[(o, n)][:].bitcast(F32)[:, 512 * q:512 * (q + 1)].rearrange("p (rr b u) -> p rr b u", rr=2, u=2)
            if engine == "s":
                nc.scalar.copy(out=dst, in_=pt[:].rearrange("p (rr u) b -> p rr b u", u=2))
            else:
                nc.vector.tensor_copy(out=dst, in_=pt[:].rearrange("p (rr u) b -> p rr b u", u=2))

        def quantise_rows(o, n, q):
            half = slice(2 * P * q, 2 * P * (q + 1))
            nc.vector.quantize_mx(out=a_codes[(o, n)][:, half].bitcast(FP8X4), scales=a_scales[(o, n)][:, half], in_=a_grouped[(o, n)][:, 8 * P * q:8 * P * (q + 1)])

        idle = psum.tile([P, TPC * P], F32, name="idle", tag="zo", bufs=2)

        def warm_up(times):
            for repeat in range(times):
                nc.tensor.matmul(idle[:], lhsT=zeros[:, 0:P], rhs=zeros[:], start=True, stop=True)

        w_grouped = {}
        w_codes = {}
        w_scales = {}

        def regroup(gate, half, engine, w=None):
            if not w:
                w_grouped[(gate, half)] = wgp.tile([P, 4 * P, 4], BF16, name="wg%d%d" % (gate, half), tag="wg", align_bytes=64)
                w_codes[(gate, half)] = codes.tile([P, 4 * P], U32, name="wcode%d%d" % (gate, half), align_bytes=64)
                w_scales[(gate, half)] = codes.tile([P, 4 * P], U8, name="wscale%d%d" % (gate, half), align_bytes=64)
            cols = slice(0, 4 * P) if w is None else slice(2 * P * w, 2 * P * (w + 1))
            dst = w_grouped[(gate, half)][:, cols, :].rearrange("p (cc i) t -> p cc t i", i=RUN)
            src = wraw[(gate, half)][:].rearrange("p t w (cm i) -> p (w cm) t i", i=RUN)[:, cols.start // RUN:cols.stop // RUN]
            if engine == "s":
                nc.scalar.copy(out=dst, in_=src)
            else:
                nc.vector.tensor_copy(out=dst, in_=src)

        def quantise_weights(gate, half, w=None):
            cols = slice(0, 4 * P) if w is None else slice(2 * P * w, 2 * P * (w + 1))
            nc.vector.quantize_mx(out=w_codes[(gate, half)][:, cols].bitcast(FP8X4), scales=w_scales[(gate, half)][:, cols], in_=w_grouped[(gate, half)][:, cols, :].rearrange("p cm t -> p (cm t)"))

        staged = {}
        for n in range(NCHUNK):
            staged[n] = [stage.tile([P, TPC, H], F32, name="stage%d%d" % (which, n)) for which in range(2)]
        accs = {}
        acts = {}
        cts = {}
        kept = {}
        news = {}
        c02s = {}
        zss = {}
        zos = {}
        tcns = {}
        hn8s = {}

        def mx_pass(n, j, gate, w):
            cols = slice(P * (2 * w + j % 2), P * (2 * w + j % 2 + 1))
            if w == 0:
                accs[(n, j, gate)] = psum.tile([P, TPC * P], F32, name="acc", tag="acc", bufs=3)
            nc.tensor.matmul_mx(
                out=accs[(n, j, gate)][:],
                lhsT=w_codes[(gate, j // 2)][:, cols].bitcast(FP8X4),
                lhsT_scale=w_scales[(gate, j // 2)][:, cols],
                rhs=a_codes[(w, n)][:].bitcast(FP8X4),
                rhs_scale=a_scales[(w, n)][:],
                start=(w == 0),
                stop=(w == 1),
            )

        def gate_act(n, j, gate):
            if j % 2 == 0:
                acts[(n, j // 2, gate)] = work.tile([P, 2, TPC * P], F32, name="act_%s" % TAG[gate], tag="act_%s" % TAG[gate], bufs=2)
            col = 4 * gate + j
            nc.scalar.activation(out=acts[(n, j // 2, gate)][:, j % 2, :], in_=accs[(n, j, gate)][:], func=FUNC[gate], bias=bias_col[:, col:col + 1], scale=1.0)

        def turn_cells(n, half):
            ct = psum.tile([P, 2, TPC * P], BF16, name="ct", tag="ct")
            for i in range(2):
                for s in range(TPC):
                    nc.tensor.transpose(ct[:, i, P * s:P * (s + 1)], sb[(CELL, n)][:, s, P * (2 * half + i):P * (2 * half + i + 1)], ident_b[:])
            cts[(n, half)] = ct

        def keep(n, half, i=None):
            which = slice(0, 2) if i is None else slice(i, i + 1)
            if not i:
                kept[(n, half)] = work.tile([P, 2, TPC * P], F32, name="keep", tag="keep", bufs=2)
            nc.vector.tensor_tensor(out=kept[(n, half)][:, which, :], in0=acts[(n, half, GATE_F)][:, which, :], in1=cts[(n, half)][:, which, :], op=ALU.mult)

        def new(n, half, i=None):
            engine = nc.gpsimd if half else nc.vector
            which = slice(0, 2) if i is None else slice(i, i + 1)
            if not i:
                news[(n, half)] = work.tile([P, 2, TPC * P], F32, name="new", tag="new", bufs=2)
            engine.tensor_tensor(out=news[(n, half)][:, which, :], in0=acts[(n, half, GATE_I)][:, which, :], in1=acts[(n, half, GATE_G)][:, which, :], op=ALU.mult)

        totals = {}

        def total(n, half, i=None):
            which = slice(0, 2) if i is None else slice(i, i + 1)
            t = work.tile([P, 2, TPC * P], F32, name="total", tag="total", bufs=1)
            nc.gpsimd.tensor_tensor(out=t[:, which, :], in0=kept[(n, half)][:, which, :], in1=news[(n, half)][:, which, :], op=ALU.add)
            for part in range(2)[which]:
                totals[(n, 2 * half + part)] = t

        def fifth_of_cell(n, half, engine):
            t = work.tile([P, TPC, 2 * P], F32, name="c02", tag="c02", bufs=3)
            src = sb[(CELL, n)][:, :, 2 * P * half:2 * P * (half + 1)]
            if engine == "s":
                nc.scalar.activation(out=t[:], in_=src, func=ACT.Copy, scale=0.2)
            else:
                nc.gpsimd.tensor_scalar(out=t[:], in0=src, scalar1=0.2, scalar2=0.0, op0=ALU.mult, op1=ALU.add)
            c02s[(n, half)] = t

        def sums(n, j, rows):
            zs = psum.tile([P, TPC, P], F32, name="zs", tag="zs", bufs=2)
            nc.tensor.matmul(zs[:, rows, :], lhsT=ident_b[:], rhs=sb[(MEM, n)][:, rows, P * j:P * (j + 1)], start=True, stop=False)
            parts = [totals[(n, j)]] if (n, j) in totals else [kept[(n, j // 2)], news[(n, j // 2)]]
            for s in range(TPC)[rows]:
                for part in parts:
                    last = s == rows.stop - 1 and part is parts[-1]
                    nc.tensor.matmul(zs[:, s, :], lhsT=part[:, j % 2, P * s:P * (s + 1)], rhs=ident_f[:], is_transpose=True, start=False, stop=last)
            zss[(n, j, rows.start)] = zs

        def turn_output_gate(n, j, rows):
            zo = psum.tile([P, TPC, P], F32, name="zo", tag="zo", bufs=2)
            for s in range(TPC)[rows]:
                nc.tensor.transpose(zo[:, s, :], acts[(n, j // 2, GATE_O)][:, j % 2, P * s:P * (s + 1)], ident_f[:])
            zos[(n, j, rows.start)] = zo

        def tanh_cell(n, j, rows):
            t = work.tile([P, TPC, P], F32, name="tcn", tag="tcn")
            nc.scalar.activation(out=t[:, rows, :], in_=zss[(n, j, rows.start)][:, rows, :], func=ACT.Tanh)
            tcns[(n, j, rows.start)] = t

        def store(which, n, cols, rows=ALL):
            nc.sync.dma_start(out=outs[which][:, TPC * n + rows.start:TPC * n + rows.stop, cols], in_=staged[n][which][:, rows, cols])

        def cell_out(n, j, alone=False, rows=ALL):
            cols = slice(P * j, P * (j + 1))
            inner = slice(P * (j % 2), P * (j % 2 + 1))
            nc.vector.scalar_tensor_tensor(out=staged[n][1][:, rows, cols], in0=zss[(n, j, rows.start)][:, rows, :], scalar=0.8, in1=c02s[(n, j // 2)][:, rows, inner], op0=ALU.mult, op1=ALU.add)
            if alone:
                store(1, n, cols, rows)
            elif j % 2 == 1:
                store(1, n, slice(P * (j - 1), P * (j + 1)))

        def hidden_part(n, j, rows=ALL):
            if (n, j // 2) not in hn8s:
                hn8s[(n, j // 2)] = work.tile([P, TPC, 2 * P], F32, name="hn8", tag="hn8", bufs=2)
            inner = slice(P * (j % 2), P * (j % 2 + 1))
            nc.vector.scalar_tensor_tensor(out=hn8s[(n, j // 2)][:, rows, inner], in0=zos[(n, j, rows.start)][:, rows, :], scalar=0.8, in1=tcns[(n, j, rows.start)][:, rows, :], op0=ALU.mult, op1=ALU.mult)

        def hidden_out(n, half, i=None, rows=ALL):
            cols = slice(2 * P * half, 2 * P * (half + 1)) if i is None else slice(P * (2 * half + i), P * (2 * half + i + 1))
            inner = slice(0, 2 * P) if i is None else slice(P * i, P * (i + 1))
            nc.vector.scalar_tensor_tensor(out=staged[n][0][:, rows, cols], in0=sb[(HID, n)][:, rows, cols], scalar=0.2, in1=hn8s[(n, half)][:, rows, inner], op0=ALU.mult, op1=ALU.add)
            store(0, n, cols, rows)

        def mx(n, half, gate):
            for j in (2 * half, 2 * half + 1):
                mx_pass(n, j, gate, 0)
                mx_pass(n, j, gate, 1)
                gate_act(n, j, gate)

        def mx1(n, j, gate):
            mx_pass(n, j, gate, 0)
            mx_pass(n, j, gate, 1)
            gate_act(n, j, gate)

        def turn_both(o, n):
            for q in range(2):
                turn_rows(o, n, q)

        def quantise_both(o, n):
            for q in range(2):
                quantise_rows(o, n, q)

        def stage_one(n, j, rows=ALL):
            sums(n, j, rows)
            turn_output_gate(n, j, rows)
            tanh_cell(n, j, rows)

        bias_t = psum.tile([P, P], BF16, name="bias_t", tag="ct")
        warm_up(4)
        turn_both(X, 0)
        nc.tensor.transpose(bias_t[:], bias_rows[:], ident_b[:])
        warm_up(2)
        regroup(GATE_F, 0, "v", 0)
        quantise_both(X, 0)
        quantise_weights(GATE_F, 0, 0)
        bias_col = const.tile([P, 16], F32, name="bias_col")
        nc.vector.tensor_copy(out=bias_col[:], in_=bias_t[:, 0:16])
        turn_both(HID, 0)
        warm_up(2)
        regroup(GATE_F, 0, "v", 1)
        quantise_both(HID, 0)
        quantise_weights(GATE_F, 0, 1)
        regroup(GATE_I, 0, "s", 0)
        regroup(GATE_I, 0, "v", 1)
        quantise_weights(GATE_I, 0)
        for w in range(2):
            for j in range(2):
                mx_pass(0, j, GATE_F, w)
        for j in range(2):
            gate_act(0, j, GATE_F)
        mx(0, 0, GATE_I)
        turn_cells(0, 0)
        for q in range(2):
            turn_rows(X, 1, q, "s", ("zs", 2))
        regroup(GATE_G, 0, "v")
        quantise_weights(GATE_G, 0)
        keep(0, 0)
        for q in range(2):
            turn_rows(HID, 1, q, "s", ("zo", 2))
        quantise_both(X, 1)
        quantise_both(HID, 1)
        regroup(GATE_O, 0, "v")
        mx(0, 0, GATE_G)
        new(0, 0)
        quantise_weights(GATE_O, 0)
        fifth_of_cell(0, 0, "s")
        mx(1, 0, GATE_F)
        turn_cells(1, 0)
        mx(1, 0, GATE_I)
        mx(0, 0, GATE_O)
        mx(1, 0, GATE_G)
        regroup(GATE_F, 1, "v")
        keep(1, 0)
        quantise_weights(GATE_F, 1)
        stage_one(0, 0)
        regroup(GATE_I, 1, "v")
        new(1, 0)
        quantise_weights(GATE_I, 1)
        mx(1, 0, GATE_O)
        stage_one(0, 1)
        regroup(GATE_G, 1, "v")
        quantise_weights(GATE_G, 1)
        cell_out(0, 0)
        hidden_part(0, 0)
        turn_cells(0, 1)
        fifth_of_cell(1, 0, "s")
        mx(0, 1, GATE_F)
        regroup(GATE_O, 1, "v")
        mx(0, 1, GATE_I)
        cell_out(0, 1)
        quantise_weights(GATE_O, 1)
        hidden_part(0, 1)
        keep(0, 1)
        mx(0, 1, GATE_G)
        stage_one(1, 0)
        mx(0, 1, GATE_O)
        stage_one(1, 1)
        hidden_out(0, 0)
        new(0, 1)
        total(0, 1)
        fifth_of_cell(0, 1, "s")
        turn_cells(1, 1)
        cell_out(1, 0)
        hidden_part(1, 0)
        cell_out(1, 1)
        hidden_part(1, 1)
        hidden_out(1, 0)
        mx1(1, 2, GATE_F)
        mx1(1, 2, GATE_I)
        mx1(1, 2, GATE_G)
        stage_one(0, 2)
        mx1(1, 2, GATE_O)
        keep(1, 1, 0)
        cell_out(0, 2)
        hidden_part(0, 2)
        new(1, 1, 0)
        fifth_of_cell(1, 1, "g")
        hidden_out(0, 1, 0)
        mx1(1, 3, GATE_F)
        mx1(1, 3, GATE_I)
        stage_one(0, 3)
        keep(1, 1, 1)
        mx1(1, 3, GATE_G)
        cell_out(0, 3)
        stage_one(1, 2)
        mx1(1, 3, GATE_O)
        hidden_part(0, 3)
        new(1, 1, 1)
        hidden_out(0, 1, 1)
        cell_out(1, 2, True)
        hidden_part(1, 2)
        hidden_out(1, 1, 0)
        halves = (slice(0, 2), slice(2, 4))
        for rows in halves:
            stage_one(1, 3, rows)
        for rows in halves:
            cell_out(1, 3, True, rows)
            hidden_part(1, 3, rows)
        for rows in halves:
            hidden_out(1, 1, 1, rows)
